import numpy as np
import ml_dtypes


def mxq(x, axis, fmt="e4m3"):
    dtype, down = {"e4m3": (ml_dtypes.float8_e4m3fn, 7), "e5m2": (ml_dtypes.float8_e5m2, 14)}[fmt]
    v = np.moveaxis(np.asarray(x, np.float32).astype(ml_dtypes.bfloat16).astype(np.float64), axis, -1)
    blocks = v.reshape(v.shape[:-1] + (-1, 32))
    amax = np.abs(blocks).max(-1, keepdims=True)
    byte = np.maximum(np.where(amax > 0, np.frexp(amax)[1] - 1 + 127, 0) - down, 1)
    scale = np.exp2(byte - 127.0)
    codes = (blocks / scale).astype(np.float32).astype(dtype).astype(np.float64)
    return np.moveaxis((codes * scale).reshape(v.shape), -1, axis)


WIDE = False


def mx_kscale(k):
    if not WIDE:
        return np.ones(k)
    levels = np.array([10, -10, 5, -5, 0])
    a = np.random.permutation(np.resize(levels, k // 512 * 4)).reshape(k // 512, 4)
    idx = np.arange(k)
    return np.exp2(a[idx // 512, idx % 128 // 32])


BF16 = ml_dtypes.bfloat16


def bf(x):
    return np.asarray(x, np.float32).astype(BF16)


def f64(x):
    return np.asarray(x).astype(np.float64)


B, C_IN, C_OUT, N, T, K = 2, 512, 128, 512, 12, 3


def cheb_laplacian(p):
    adj = 1.0 / (1.0 + np.exp(-p))
    adj = (adj + adj.T) * 0.5
    adj = adj * (1.0 - np.eye(N))
    deg = adj.sum(axis=1)
    dis = 1.0 / np.sqrt(deg)
    return -(dis[:, None] * adj * dis[None, :])


def setup_inputs():
    s = mx_kscale(C_IN)
    x = np.random.standard_normal((B, C_IN, 1, T)) + np.random.standard_normal((B, C_IN, N, T))
    return {'x': bf(x * s[None, :, None, None]),
            'adj_param': bf(4.0 * np.random.standard_normal((N, N)) - 10.0 + 10.0 * np.eye(N)),
            'w_cheb0': bf(np.random.standard_normal((C_IN, C_OUT)) / np.sqrt(C_IN) / s[:, None]),
            'w_cheb1': bf(np.random.standard_normal((C_IN, C_OUT)) / np.sqrt(C_IN) / s[:, None])}


def reference(x, adj_param, w_cheb0, w_cheb1):
    s = cheb_laplacian(f64(adj_param))
    xt = f64(x).transpose(0, 3, 2, 1)
    h = mxq(xt, 3, 'e4m3') @ mxq(f64(w_cheb0), 0, 'e4m3')
    tx1 = mxq(s, 1, 'e4m3') @ mxq(xt, 2, 'e4m3')
    h = h + (mxq(tx1, 3, 'e4m3') @ mxq(f64(w_cheb1), 0, 'e4m3'))
    return h

@@ -1,0 +1,243 @@
+from contextlib import ExitStack
+
+import concourse.mybir as mybir
+from concourse.masks import make_identity
+
+BF16 = mybir.dt.bfloat16
+F32 = mybir.dt.float32
+U32 = mybir.dt.uint32
+U8 = mybir.dt.uint8
+FP8X4 = mybir.dt.float8_e4m3fn_x4
+ACT = mybir.ActivationFunctionType
+ALU = mybir.AluOpType
+
+P = 128
+PACK = 4
+BATCH, CHANNELS, NODES, TIMES, CH_OUT = 2, 512, 512, 12, 128
+assert CHANNELS == P * PACK and NODES == P * PACK and CH_OUT == P
+
+STEPS = BATCH * TIMES
+PLANE = P * PACK * PACK
+T_GROUP = 4
+GROUPS = TIMES // T_GROUP
+CHUNKS = 4
+CHUNK_PN = P // CHUNKS
+CHUNK_COLS = CHUNK_PN * PACK * TIMES
+ITEMS = BATCH * GROUPS * CHUNKS
+
+FLOPS = 2 * STEPS * (NODES * NODES * CHANNELS + 2 * NODES * CHANNELS * CH_OUT)
+
+
+def tile_dynamicgraphspatialconv_pa_t_kernel(tc, x, adj_param, w_cheb0, w_cheb1, out):
+    nc = tc.nc
+    with ExitStack() as ctx:
+        const = ctx.enter_context(tc.tile_pool(name="const", bufs=1))
+        prep = ctx.enter_context(tc.tile_pool(name="prep", bufs=1))
+        raw_pool = ctx.enter_context(tc.tile_pool(name="raw", bufs=CHUNKS))
+        gc_pool = ctx.enter_context(tc.tile_pool(name="gc", bufs=3))
+        xc_pool = ctx.enter_context(tc.tile_pool(name="xc", bufs=4))
+        work = ctx.enter_context(tc.tile_pool(name="work", bufs=2))
+        store = ctx.enter_context(tc.tile_pool(name="store", bufs=3))
+        tr_psum = ctx.enter_context(tc.psum_pool(name="tr_psum", bufs=2))
+        tx_psum = ctx.enter_context(tc.psum_pool(name="tx_psum", bufs=4))
+        o_psum = ctx.enter_context(tc.psum_pool(name="o_psum", bufs=2))
+
+        adj_raw = prep.tile([P, PACK, NODES], BF16, name="adj_raw")
+        nc.sync.dma_start(out=adj_raw[:], in_=adj_param.rearrange("(p q) m -> p q m", q=PACK))
+        w_raw = prep.tile([P, 2, PACK, CH_OUT], BF16, name="w_raw")
+        nc.scalar.dma_start(out=w_raw[:, 0], in_=w_cheb0.rearrange("(p j) o -> p j o", j=PACK))
+        nc.scalar.dma_start(out=w_raw[:, 1], in_=w_cheb1.rearrange("(p j) o -> p j o", j=PACK))
+
+        raw_tiles = {}
+
+        def load_chunk(b, h):
+            raw = raw_pool.tile([P, PACK, CHUNK_COLS], BF16, name="raw")
+            channels_first = x[b].rearrange("(p j) n t -> p j (n t)", j=PACK)
+            nc.sync.dma_start(out=raw[:], in_=channels_first[:, :, h * CHUNK_COLS : (h + 1) * CHUNK_COLS])
+            raw_tiles[(b, h)] = raw
+
+        for h in range(CHUNKS):
+            load_chunk(0, h)
+
+        ident = const.tile([P, P], F32, name="ident")
+        make_identity(nc, ident[:])
+        off_diagonal = const.tile([P, P], F32, name="off_diagonal")
+        nc.vector.tensor_scalar(
+            out=off_diagonal[:], in0=ident[:], scalar1=-1.0, scalar2=1.0, op0=ALU.mult, op1=ALU.add
+        )
+
+        w_grouped = prep.tile([P, 2, CH_OUT, PACK], BF16, name="w_grouped", align_bytes=64)
+        nc.vector.tensor_copy(out=w_grouped[:], in_=w_raw[:].rearrange("p w j o -> p w o j"))
+        w_codes = const.tile([P, 2 * CH_OUT], U32, name="w_codes", align_bytes=64)
+        w_scales = const.tile([P, 2 * CH_OUT], U8, name="w_scales", align_bytes=64)
+        nc.vector.quantize_mx(
+            out=w_codes[:].bitcast(FP8X4),
+            scales=w_scales[:],
+            in_=w_grouped[:].rearrange("p w o j -> p (w o j)"),
+        )
+
+        a = prep.tile([P, PACK, PACK, P], F32, name="a")
+        for q in range(PACK):
+            nc.scalar.activation(
+                out=a[:, q],
+                in_=adj_raw[:, q, :].rearrange("p (c k) -> p k c", k=PACK),
+                func=ACT.Sigmoid,
+            )
+            nc.vector.tensor_tensor(out=a[:, q, q, :], in0=a[:, q, q, :], in1=off_diagonal[:], op=ALU.mult)
+        two_a = prep.tile([P, PACK, PACK * P], F32, name="two_a")
+        for k in range(PACK):
+            a_t = tx_psum.tile([P, PACK, P], F32, name="tx")
+            for q in range(PACK):
+                nc.tensor.transpose(a_t[:, q, :], a[:, q, k, :], ident[:])
+            nc.vector.tensor_tensor(
+                out=two_a[:, k, :],
+                in0=a[:, k].rearrange("p k c -> p (k c)"),
+                in1=a_t[:].rearrange("p q c -> p (q c)"),
+                op=ALU.add,
+            )
+        two_deg = prep.tile([P, PACK], F32, name="two_deg")
+        nc.vector.tensor_reduce(out=two_deg[:], in_=two_a[:], axis=mybir.AxisListType.X, op=ALU.add)
+        root = prep.tile([P, PACK], F32, name="root")
+        nc.scalar.activation(out=root[:], in_=two_deg[:], func=ACT.Sqrt, scale=0.5)
+        inv_root = prep.tile([P, PACK], F32, name="inv_root")
+        nc.vector.reciprocal(out=inv_root[:], in_=root[:])
+        row_factor = prep.tile([P, PACK], F32, name="row_factor")
+        nc.vector.tensor_scalar(out=row_factor[:], in0=inv_root[:], scalar1=-0.5, scalar2=None, op0=ALU.mult)
+        repeated = prep.tile([P, PACK, P], F32, name="repeated")
+        nc.vector.tensor_copy(out=repeated[:], in_=inv_root[:].unsqueeze(2).to_broadcast([P, PACK, P]))
+        column_factor = o_psum.tile([P, PACK, P], F32, name="o_ps")
+        for k in range(PACK):
+            nc.tensor.transpose(column_factor[:, k, :], repeated[:, k, :], ident[:])
+        nc.vector.tensor_tensor(
+            out=two_a[:],
+            in0=two_a[:],
+            in1=row_factor[:].unsqueeze(2).to_broadcast([P, PACK, PACK * P]),
+            op=ALU.mult,
+        )
+        s_grouped = prep.tile([P, PACK * P, PACK], BF16, name="s_grouped", align_bytes=64)
+        nc.vector.tensor_tensor(
+            out=s_grouped[:],
+            in0=two_a[:].rearrange("p q v -> p v q"),
+            in1=column_factor[:].rearrange("p k c -> p (k c)").unsqueeze(2).to_broadcast([P, PACK * P, PACK]),
+            op=ALU.mult,
+        )
+        s_codes = const.tile([P, PACK * P], U32, name="s_codes", align_bytes=64)
+        s_scales = const.tile([P, PACK * P], U8, name="s_scales", align_bytes=64)
+        nc.vector.quantize_mx(
+            out=s_codes[:].bitcast(FP8X4), scales=s_scales[:], in_=s_grouped[:].rearrange("p v q -> p (v q)")
+        )
+
+        gc_tiles = {}
+        xc, gn, xn, tx, gt, t1 = {}, {}, {}, {}, {}, {}
+
+        def regroup(item):
+            group, h = divmod(item, CHUNKS)
+            b, g = divmod(group, GROUPS)
+            if h == 0:
+                gc_tiles[group] = gc_pool.tile([P, T_GROUP * PLANE], BF16, name="gc", align_bytes=64)
+            planes = gc_tiles[group][:].rearrange("p (t q n j) -> p q n j t", t=T_GROUP, q=PACK, n=P, j=PACK)
+            piece = raw_tiles[(b, h)][:].rearrange("p j (n q t) -> p q n j t", q=PACK, t=TIMES)
+            nc.vector.tensor_copy(
+                out=planes[:, :, h * CHUNK_PN : (h + 1) * CHUNK_PN, :, :],
+                in_=piece[:, :, :, :, g * T_GROUP : (g + 1) * T_GROUP],
+            )
+
+        def channel_plane(i):
+            group, t = divmod(i, T_GROUP)
+            return gc_tiles[group][:, t * PLANE : (t + 1) * PLANE]
+
+        def quantise(pool, name, grouped):
+            codes = pool.tile([P, PACK * P], U32, name=name + "_codes", align_bytes=64)
+            scales = pool.tile([P, PACK * P], U8, name=name + "_scales", align_bytes=64)
+            nc.vector.quantize_mx(out=codes[:].bitcast(FP8X4), scales=scales[:], in_=grouped)
+            return codes, scales
+
+        def transpose_to_nodes(i):
+            words = channel_plane(i).bitcast(F32).rearrange("p (q n h) -> p q n h", q=PACK, n=P, h=2)
+            gn[i] = work.tile([P, PLANE], BF16, name="gn", align_bytes=64)
+            for h in range(2):
+                tr = tr_psum.tile([P, PACK, P], F32, name="tr")
+                for q in range(PACK):
+                    nc.tensor.transpose(tr[:, q, :], words[:, q, :, h], ident[:])
+                nc.scalar.copy(
+                    out=gn[i][:, h * PLANE // 2 : (h + 1) * PLANE // 2].rearrange(
+                        "p (e c q) -> p e c q", e=2, c=P, q=PACK
+                    ),
+                    in_=tr[:].rearrange("p q c -> p (q c)").bitcast(BF16).rearrange(
+                        "p (q c e) -> p e c q", q=PACK, c=P, e=2
+                    ),
+                )
+
+        def multiply_by_graph(i):
+            codes, scales = xn[i]
+            tx[i] = []
+            for v_block in range(PACK):
+                bank = tx_psum.tile([P, PACK, P], F32, name="tx")
+                v_cols = slice(v_block * P, (v_block + 1) * P)
+                for j in range(PACK):
+                    c_cols = slice(j * P, (j + 1) * P)
+                    nc.tensor.matmul_mx(
+                        out=bank[:, j, :],
+                        lhsT=codes[:, c_cols].bitcast(FP8X4),
+                        lhsT_scale=scales[:, c_cols],
+                        rhs=s_codes[:, v_cols].bitcast(FP8X4),
+                        rhs_scale=s_scales[:, v_cols],
+                        start=True,
+                        stop=True,
+                    )
+                tx[i].append(bank)
+
+        def round_tx1(i):
+            gt[i] = work.tile([P, PLANE], BF16, name="gt", align_bytes=64)
+            for v_block in range(PACK):
+                copy = nc.vector.tensor_copy if v_block < PACK // 2 else nc.scalar.copy
+                copy(
+                    out=gt[i][:, v_block * P * PACK : (v_block + 1) * P * PACK].rearrange("p (v j) -> p v j", j=PACK),
+                    in_=tx[i][v_block][:].rearrange("p j v -> p v j"),
+                )
+
+        def project(i):
+            b, t = divmod(i, TIMES)
+            o_ps = o_psum.tile([P, PACK, CH_OUT], F32, name="o_ps")
+            for q in range(PACK):
+                n_cols = slice(q * P, (q + 1) * P)
+                for order, (codes, scales) in enumerate((xc[i], t1[i])):
+                    o_cols = slice(order * CH_OUT, (order + 1) * CH_OUT)
+                    nc.tensor.matmul_mx(
+                        out=o_ps[:, q, :],
+                        lhsT=codes[:, n_cols].bitcast(FP8X4),
+                        lhsT_scale=scales[:, n_cols],
+                        rhs=w_codes[:, o_cols].bitcast(FP8X4),
+                        rhs_scale=w_scales[:, o_cols],
+                        start=(order == 0),
+                        stop=(order == 1),
+                    )
+            o_sb = store.tile([P, PACK * CH_OUT], F32, name="o_sb")
+            nc.scalar.copy(out=o_sb[:], in_=o_ps[:].rearrange("p q o -> p (q o)"))
+            nc.sync.dma_start(out=out[b, t].rearrange("(p q) o -> p (q o)", q=PACK), in_=o_sb[:])
+
+        AHEAD = CHUNKS + 2
+        for item in range(CHUNKS):
+            regroup(item)
+        for step in range(-2, STEPS):
+            first, second, third = step + 2, step + 1, step
+            if 0 <= second < STEPS:
+                xn[second] = quantise(work, "xn", gn[second][:])
+            if 0 <= third:
+                t1[third] = quantise(work, "t1", gt[third][:])
+            if first < STEPS:
+                transpose_to_nodes(first)
+            if 0 <= second < STEPS:
+                multiply_by_graph(second)
+            if first < STEPS:
+                xc[first] = quantise(xc_pool, "xc", channel_plane(first))
+            if 0 <= second < STEPS:
+                round_tx1(second)
+            if 0 <= third:
+                project(third)
+            item = step + AHEAD
+            if item < ITEMS:
+                regroup(item)
+                group, h = divmod(item, CHUNKS)
+                if group == GROUPS - 1:
+                    load_chunk(1, h)

@@ -34,13 +34,13 @@ def tile_dynamicgraphspatialconv_pa_t_kernel(tc, x, adj_param, w_cheb0, w_cheb1,
         const = ctx.enter_context(tc.tile_pool(name="const", bufs=1))
         prep = ctx.enter_context(tc.tile_pool(name="prep", bufs=1))
         raw_pool = ctx.enter_context(tc.tile_pool(name="raw", bufs=CHUNKS))
-        gc_pool = ctx.enter_context(tc.tile_pool(name="gc", bufs=3))
+        gc_pool = ctx.enter_context(tc.tile_pool(name="gc", bufs=4))
         xc_pool = ctx.enter_context(tc.tile_pool(name="xc", bufs=4))
-        work = ctx.enter_context(tc.tile_pool(name="work", bufs=2))
+        work = ctx.enter_context(tc.tile_pool(name="work", bufs=3))
         store = ctx.enter_context(tc.tile_pool(name="store", bufs=3))
-        tr_psum = ctx.enter_context(tc.psum_pool(name="tr_psum", bufs=2))
+        tr_psum = ctx.enter_context(tc.psum_pool(name="tr_psum", bufs=3))
         tx_psum = ctx.enter_context(tc.psum_pool(name="tx_psum", bufs=4))
-        o_psum = ctx.enter_context(tc.psum_pool(name="o_psum", bufs=2))
+        o_psum = ctx.enter_context(tc.psum_pool(name="o_psum", bufs=1))
 
         adj_raw = prep.tile([P, PACK, NODES], BF16, name="adj_raw")
         nc.sync.dma_start(out=adj_raw[:], in_=adj_param.rearrange("(p q) m -> p q m", q=PACK))
@@ -58,74 +58,6 @@ def tile_dynamicgraphspatialconv_pa_t_kernel(tc, x, adj_param, w_cheb0, w_cheb1,
 
         for h in range(CHUNKS):
             load_chunk(0, h)
-
-        ident = const.tile([P, P], F32, name="ident")
-        make_identity(nc, ident[:])
-        off_diagonal = const.tile([P, P], F32, name="off_diagonal")
-        nc.vector.tensor_scalar(
-            out=off_diagonal[:], in0=ident[:], scalar1=-1.0, scalar2=1.0, op0=ALU.mult, op1=ALU.add
-        )
-
-        w_grouped = prep.tile([P, 2, CH_OUT, PACK], BF16, name="w_grouped", align_bytes=64)
-        nc.vector.tensor_copy(out=w_grouped[:], in_=w_raw[:].rearrange("p w j o -> p w o j"))
-        w_codes = const.tile([P, 2 * CH_OUT], U32, name="w_codes", align_bytes=64)
-        w_scales = const.tile([P, 2 * CH_OUT], U8, name="w_scales", align_bytes=64)
-        nc.vector.quantize_mx(
-            out=w_codes[:].bitcast(FP8X4),
-            scales=w_scales[:],
-            in_=w_grouped[:].rearrange("p w o j -> p (w o j)"),
-        )
-
-        a = prep.tile([P, PACK, PACK, P], F32, name="a")
-        for q in range(PACK):
-            nc.scalar.activation(
-                out=a[:, q],
-                in_=adj_raw[:, q, :].rearrange("p (c k) -> p k c", k=PACK),
-                func=ACT.Sigmoid,
-            )
-            nc.vector.tensor_tensor(out=a[:, q, q, :], in0=a[:, q, q, :], in1=off_diagonal[:], op=ALU.mult)
-        two_a = prep.tile([P, PACK, PACK * P], F32, name="two_a")
-        for k in range(PACK):
-            a_t = tx_psum.tile([P, PACK, P], F32, name="tx")
-            for q in range(PACK):
-                nc.tensor.transpose(a_t[:, q, :], a[:, q, k, :], ident[:])
-            nc.vector.tensor_tensor(
-                out=two_a[:, k, :],
-                in0=a[:, k].rearrange("p k c -> p (k c)"),
-                in1=a_t[:].rearrange("p q c -> p (q c)"),
-                op=ALU.add,
-            )
-        two_deg = prep.tile([P, PACK], F32, name="two_deg")
-        nc.vector.tensor_reduce(out=two_deg[:], in_=two_a[:], axis=mybir.AxisListType.X, op=ALU.add)
-        root = prep.tile([P, PACK], F32, name="root")
-        nc.scalar.activation(out=root[:], in_=two_deg[:], func=ACT.Sqrt, scale=0.5)
-        inv_root = prep.tile([P, PACK], F32, name="inv_root")
-        nc.vector.reciprocal(out=inv_root[:], in_=root[:])
-        row_factor = prep.tile([P, PACK], F32, name="row_factor")
-        nc.vector.tensor_scalar(out=row_factor[:], in0=inv_root[:], scalar1=-0.5, scalar2=None, op0=ALU.mult)
-        repeated = prep.tile([P, PACK, P], F32, name="repeated")
-        nc.vector.tensor_copy(out=repeated[:], in_=inv_root[:].unsqueeze(2).to_broadcast([P, PACK, P]))
-        column_factor = o_psum.tile([P, PACK, P], F32, name="o_ps")
-        for k in range(PACK):
-            nc.tensor.transpose(column_factor[:, k, :], repeated[:, k, :], ident[:])
-        nc.vector.tensor_tensor(
-            out=two_a[:],
-            in0=two_a[:],
-            in1=row_factor[:].unsqueeze(2).to_broadcast([P, PACK, PACK * P]),
-            op=ALU.mult,
-        )
-        s_grouped = prep.tile([P, PACK * P, PACK], BF16, name="s_grouped", align_bytes=64)
-        nc.vector.tensor_tensor(
-            out=s_grouped[:],
-            in0=two_a[:].rearrange("p q v -> p v q"),
-            in1=column_factor[:].rearrange("p k c -> p (k c)").unsqueeze(2).to_broadcast([P, PACK * P, PACK]),
-            op=ALU.mult,
-        )
-        s_codes = const.tile([P, PACK * P], U32, name="s_codes", align_bytes=64)
-        s_scales = const.tile([P, PACK * P], U8, name="s_scales", align_bytes=64)
-        nc.vector.quantize_mx(
-            out=s_codes[:].bitcast(FP8X4), scales=s_scales[:], in_=s_grouped[:].rearrange("p v q -> p (v q)")
-        )
 
         gc_tiles = {}
         xc, gn, xn, tx, gt, t1 = {}, {}, {}, {}, {}, {}
@@ -216,9 +148,84 @@ def tile_dynamicgraphspatialconv_pa_t_kernel(tc, x, adj_param, w_cheb0, w_cheb1,
             nc.scalar.copy(out=o_sb[:], in_=o_ps[:].rearrange("p q o -> p (q o)"))
             nc.sync.dma_start(out=out[b, t].rearrange("(p q) o -> p (q o)", q=PACK), in_=o_sb[:])
 
+        with tc.manual_schedule():
+            ident = const.tile([P, P], F32, name="ident")
+            make_identity(nc, ident[:])
+            off_diagonal = const.tile([P, P], F32, name="off_diagonal")
+            nc.vector.tensor_scalar(
+                out=off_diagonal[:], in0=ident[:], scalar1=-1.0, scalar2=1.0, op0=ALU.mult, op1=ALU.add
+            )
+            one = prep.tile([P, 1], F32, name="one")
+            nc.vector.memset(one[:], 1.0)
+
+            w_grouped = prep.tile([P, 2, CH_OUT, PACK], BF16, name="w_grouped", align_bytes=64)
+            nc.vector.tensor_copy(out=w_grouped[:], in_=w_raw[:].rearrange("p w j o -> p w o j"))
+            w_codes = const.tile([P, 2 * CH_OUT], U32, name="w_codes", align_bytes=64)
+            w_scales = const.tile([P, 2 * CH_OUT], U8, name="w_scales", align_bytes=64)
+
+            a = prep.tile([P, PACK, PACK, P], F32, name="a")
+            for q in range(PACK):
+                nc.scalar.activation(
+                    out=a[:, q],
+                    in_=adj_raw[:, q, :].rearrange("p (c k) -> p k c", k=PACK),
+                    func=ACT.Sigmoid,
+                )
+                nc.vector.tensor_tensor(out=a[:, q, q, :], in0=a[:, q, q, :], in1=off_diagonal[:], op=ALU.mult)
+            warm = prep.tile([P, 1], F32, name="warm")
+            nc.scalar.activation(out=warm[:], in_=one[:], func=ACT.Sqrt)
+            nc.vector.quantize_mx(
+                out=w_codes[:].bitcast(FP8X4),
+                scales=w_scales[:],
+                in_=w_grouped[:].rearrange("p w o j -> p (w o j)"),
+            )
+            two_a = prep.tile([P, PACK, PACK * P], F32, name="two_a")
+            two_deg = prep.tile([P, PACK], F32, name="two_deg")
+            for k in range(PACK):
+                a_t = tx_psum.tile([P, PACK, P], F32, name="tx")
+                for q in range(PACK):
+                    nc.tensor.transpose(a_t[:, q, :], a[:, q, k, :], ident[:])
+                nc.vector.tensor_tensor(
+                    out=two_a[:, k, :],
+                    in0=a[:, k].rearrange("p k c -> p (k c)"),
+                    in1=a_t[:].rearrange("p q c -> p (q c)"),
+                    op=ALU.add,
+                )
+                nc.scalar.activation(
+                    out=two_a[:, k, :], in_=two_a[:, k, :], func=ACT.Copy, accum_out=two_deg[:, k : k + 1]
+                )
+            regroup(0)
+            root = prep.tile([P, PACK], F32, name="root")
+            nc.scalar.activation(out=root[:], in_=two_deg[:], func=ACT.Sqrt, scale=0.5)
+            inv_root = prep.tile([P, PACK], F32, name="inv_root")
+            nc.vector.reciprocal(out=inv_root[:], in_=root[:])
+            row_factor = prep.tile([P, PACK], F32, name="row_factor")
+            nc.vector.tensor_scalar(out=row_factor[:], in0=inv_root[:], scalar1=-0.5, scalar2=None, op0=ALU.mult)
+            for q in range(PACK):
+                nc.scalar.activation(
+                    out=two_a[:, q, :], in_=two_a[:, q, :], func=ACT.Copy, scale=row_factor[:, q : q + 1]
+                )
+            repeated = prep.tile([P, PACK, P], F32, name="repeated")
+            nc.vector.tensor_copy(out=repeated[:], in_=inv_root[:].unsqueeze(2).to_broadcast([P, PACK, P]))
+            column_factor = o_psum.tile([P, PACK, P], F32, name="o_ps")
+            for k in range(PACK):
+                nc.tensor.transpose(column_factor[:, k, :], repeated[:, k, :], ident[:])
+            regroup(1)
+            s_grouped = prep.tile([P, PACK * P, PACK], BF16, name="s_grouped", align_bytes=64)
+            nc.vector.tensor_tensor(
+                out=s_grouped[:],
+                in0=two_a[:].rearrange("p q v -> p v q"),
+                in1=column_factor[:].rearrange("p k c -> p (k c)").unsqueeze(2).to_broadcast([P, PACK * P, PACK]),
+                op=ALU.mult,
+            )
+            regroup(2)
+            s_codes = const.tile([P, PACK * P], U32, name="s_codes", align_bytes=64)
+            s_scales = const.tile([P, PACK * P], U8, name="s_scales", align_bytes=64)
+            nc.vector.quantize_mx(
+                out=s_codes[:].bitcast(FP8X4), scales=s_scales[:], in_=s_grouped[:].rearrange("p v q -> p (v q)")
+            )
+            regroup(3)
+
         AHEAD = CHUNKS + 2
-        for item in range(CHUNKS):
-            regroup(item)
         for step in range(-2, STEPS):
             first, second, third = step + 2, step + 1, step
             if 0 <= second < STEPS:

@@ -24,6 +24,7 @@ CHUNKS = 4
 CHUNK_PN = P // CHUNKS
 CHUNK_COLS = CHUNK_PN * PACK * TIMES
 ITEMS = BATCH * GROUPS * CHUNKS
+AHEAD = CHUNKS + 2
 
 FLOPS = 2 * STEPS * (NODES * NODES * CHANNELS + 2 * NODES * CHANNELS * CH_OUT)
 
@@ -44,9 +45,6 @@ def tile_dynamicgraphspatialconv_pa_t_kernel(tc, x, adj_param, w_cheb0, w_cheb1,
 
         adj_raw = prep.tile([P, PACK, NODES], BF16, name="adj_raw")
         nc.sync.dma_start(out=adj_raw[:], in_=adj_param.rearrange("(p q) m -> p q m", q=PACK))
-        w_raw = prep.tile([P, 2, PACK, CH_OUT], BF16, name="w_raw")
-        nc.scalar.dma_start(out=w_raw[:, 0], in_=w_cheb0.rearrange("(p j) o -> p j o", j=PACK))
-        nc.scalar.dma_start(out=w_raw[:, 1], in_=w_cheb1.rearrange("(p j) o -> p j o", j=PACK))
 
         raw_tiles = {}
 
@@ -58,6 +56,9 @@ def tile_dynamicgraphspatialconv_pa_t_kernel(tc, x, adj_param, w_cheb0, w_cheb1,
 
         for h in range(CHUNKS):
             load_chunk(0, h)
+        w_raw = prep.tile([P, 2, PACK, CH_OUT], BF16, name="w_raw")
+        nc.sync.dma_start(out=w_raw[:, 0], in_=w_cheb0.rearrange("(p j) o -> p j o", j=PACK))
+        nc.sync.dma_start(out=w_raw[:, 1], in_=w_cheb1.rearrange("(p j) o -> p j o", j=PACK))
 
         gc_tiles = {}
         xc, gn, xn, tx, gt, t1 = {}, {}, {}, {}, {}, {}
@@ -121,8 +122,9 @@ def tile_dynamicgraphspatialconv_pa_t_kernel(tc, x, adj_param, w_cheb0, w_cheb1,
 
         def round_tx1(i):
             gt[i] = work.tile([P, PLANE], BF16, name="gt", align_bytes=64)
+            vector_banks = 2 if i - 1 + AHEAD < ITEMS else 3
             for v_block in range(PACK):
-                copy = nc.vector.tensor_copy if v_block < PACK // 2 else nc.scalar.copy
+                copy = nc.vector.tensor_copy if v_block < vector_banks else nc.scalar.copy
                 copy(
                     out=gt[i][:, v_block * P * PACK : (v_block + 1) * P * PACK].rearrange("p (v j) -> p v j", j=PACK),
                     in_=tx[i][v_block][:].rearrange("p j v -> p v j"),
@@ -158,11 +160,6 @@ def tile_dynamicgraphspatialconv_pa_t_kernel(tc, x, adj_param, w_cheb0, w_cheb1,
             one = prep.tile([P, 1], F32, name="one")
             nc.vector.memset(one[:], 1.0)
 
-            w_grouped = prep.tile([P, 2, CH_OUT, PACK], BF16, name="w_grouped", align_bytes=64)
-            nc.vector.tensor_copy(out=w_grouped[:], in_=w_raw[:].rearrange("p w j o -> p w o j"))
-            w_codes = const.tile([P, 2 * CH_OUT], U32, name="w_codes", align_bytes=64)
-            w_scales = const.tile([P, 2 * CH_OUT], U8, name="w_scales", align_bytes=64)
-
             a = prep.tile([P, PACK, PACK, P], F32, name="a")
             for q in range(PACK):
                 nc.scalar.activation(
@@ -173,11 +170,7 @@ def tile_dynamicgraphspatialconv_pa_t_kernel(tc, x, adj_param, w_cheb0, w_cheb1,
                 nc.vector.tensor_tensor(out=a[:, q, q, :], in0=a[:, q, q, :], in1=off_diagonal[:], op=ALU.mult)
             warm = prep.tile([P, 1], F32, name="warm")
             nc.scalar.activation(out=warm[:], in_=one[:], func=ACT.Sqrt)
-            nc.vector.quantize_mx(
-                out=w_codes[:].bitcast(FP8X4),
-                scales=w_scales[:],
-                in_=w_grouped[:].rearrange("p w o j -> p (w o j)"),
-            )
+            regroup(0)
             two_a = prep.tile([P, PACK, PACK * P], F32, name="two_a")
             two_deg = prep.tile([P, PACK], F32, name="two_deg")
             for k in range(PACK):
@@ -193,7 +186,7 @@ def tile_dynamicgraphspatialconv_pa_t_kernel(tc, x, adj_param, w_cheb0, w_cheb1,
                 nc.scalar.activation(
                     out=two_a[:, k, :], in_=two_a[:, k, :], func=ACT.Copy, accum_out=two_deg[:, k : k + 1]
                 )
-            regroup(0)
+            regroup(1)
             root = prep.tile([P, PACK], F32, name="root")
             nc.scalar.activation(out=root[:], in_=two_deg[:], func=ACT.Sqrt, scale=0.5)
             inv_root = prep.tile([P, PACK], F32, name="inv_root")
@@ -209,7 +202,8 @@ def tile_dynamicgraphspatialconv_pa_t_kernel(tc, x, adj_param, w_cheb0, w_cheb1,
             column_factor = o_psum.tile([P, PACK, P], F32, name="o_ps")
             for k in range(PACK):
                 nc.tensor.transpose(column_factor[:, k, :], repeated[:, k, :], ident[:])
-            regroup(1)
+            regroup(2)
+            regroup(3)
             s_grouped = prep.tile([P, PACK * P, PACK], BF16, name="s_grouped", align_bytes=64)
             nc.vector.tensor_tensor(
                 out=s_grouped[:],
@@ -217,15 +211,21 @@ def tile_dynamicgraphspatialconv_pa_t_kernel(tc, x, adj_param, w_cheb0, w_cheb1,
                 in1=column_factor[:].rearrange("p k c -> p (k c)").unsqueeze(2).to_broadcast([P, PACK * P, PACK]),
                 op=ALU.mult,
             )
-            regroup(2)
+            w_grouped = prep.tile([P, 2, CH_OUT, PACK], BF16, name="w_grouped", align_bytes=64)
+            nc.vector.tensor_copy(out=w_grouped[:], in_=w_raw[:].rearrange("p w j o -> p w o j"))
             s_codes = const.tile([P, PACK * P], U32, name="s_codes", align_bytes=64)
             s_scales = const.tile([P, PACK * P], U8, name="s_scales", align_bytes=64)
             nc.vector.quantize_mx(
                 out=s_codes[:].bitcast(FP8X4), scales=s_scales[:], in_=s_grouped[:].rearrange("p v q -> p (v q)")
             )
-            regroup(3)
+            w_codes = const.tile([P, 2 * CH_OUT], U32, name="w_codes", align_bytes=64)
+            w_scales = const.tile([P, 2 * CH_OUT], U8, name="w_scales", align_bytes=64)
+            nc.vector.quantize_mx(
+                out=w_codes[:].bitcast(FP8X4),
+                scales=w_scales[:],
+                in_=w_grouped[:].rearrange("p w o j -> p (w o j)"),
+            )
 
-        AHEAD = CHUNKS + 2
         for step in range(-2, STEPS):
             first, second, third = step + 2, step + 1, step
             if 0 <= second < STEPS:

@@ -18,13 +18,14 @@ assert CHANNELS == P * PACK and NODES == P * PACK and CH_OUT == P
 
 STEPS = BATCH * TIMES
 PLANE = P * PACK * PACK
+BLOCK_COLS = P * TIMES
+Z_GROUPS = CHANNELS * PACK // P
+Z_LOADS = 4
+BANK_GROUPS = 8
 T_GROUP = 4
 GROUPS = TIMES // T_GROUP
-CHUNKS = 4
-CHUNK_PN = P // CHUNKS
-CHUNK_COLS = CHUNK_PN * PACK * TIMES
-ITEMS = BATCH * GROUPS * CHUNKS
-AHEAD = CHUNKS + 2
+ITEMS = BATCH * GROUPS * PACK
+LAG = 3
 
 FLOPS = 2 * STEPS * (NODES * NODES * CHANNELS + 2 * NODES * CHANNELS * CH_OUT)
 
@@ -33,51 +34,34 @@ def tile_dynamicgraphspatialconv_pa_t_kernel(tc, x, adj_param, w_cheb0, w_cheb1,
     nc = tc.nc
     with ExitStack() as ctx:
         const = ctx.enter_context(tc.tile_pool(name="const", bufs=1))
-        prep = ctx.enter_context(tc.tile_pool(name="prep", bufs=1))
-        raw_pool = ctx.enter_context(tc.tile_pool(name="raw", bufs=CHUNKS))
-        gc_pool = ctx.enter_context(tc.tile_pool(name="gc", bufs=4))
-        xc_pool = ctx.enter_context(tc.tile_pool(name="xc", bufs=4))
-        work = ctx.enter_context(tc.tile_pool(name="work", bufs=3))
+        z_pool = ctx.enter_context(tc.tile_pool(name="z0", bufs=1))
+        raw_pool = ctx.enter_context(tc.tile_pool(name="raw", bufs=PACK))
+        gc_pool = ctx.enter_context(tc.tile_pool(name="gc", bufs=3))
+        xc_pool = ctx.enter_context(tc.tile_pool(name="xc", bufs=2 * PACK + 1))
+        work = ctx.enter_context(tc.tile_pool(name="work", bufs=2))
+        t1_pool = ctx.enter_context(tc.tile_pool(name="t1", bufs=LAG + 2))
         store = ctx.enter_context(tc.tile_pool(name="store", bufs=3))
         tr_psum = ctx.enter_context(tc.psum_pool(name="tr_psum", bufs=3))
         tx_psum = ctx.enter_context(tc.psum_pool(name="tx_psum", bufs=4))
         o_psum = ctx.enter_context(tc.psum_pool(name="o_psum", bufs=1))
 
-        adj_raw = prep.tile([P, PACK, NODES], BF16, name="adj_raw")
-        nc.sync.dma_start(out=adj_raw[:], in_=adj_param.rearrange("(p q) m -> p q m", q=PACK))
+        z_tiles, raw_tiles = {}, {}
 
-        raw_tiles = {}
+        def load_z(pool, b):
+            z_tiles[b] = pool.tile([P, Z_GROUPS, BLOCK_COLS], BF16, name="z")
+            runs = x[b].rearrange("c n t -> (c n t)").rearrange("(g p f) -> p g f", g=Z_GROUPS, p=P)
+            share = Z_GROUPS // Z_LOADS
+            for k in range(Z_LOADS):
+                groups = slice(k * share, (k + 1) * share)
+                nc.sync.dma_start(out=z_tiles[b][:, groups, :], in_=runs[:, groups, :])
 
-        def load_chunk(b, h):
-            raw = raw_pool.tile([P, PACK, CHUNK_COLS], BF16, name="raw")
-            channels_first = x[b].rearrange("(p j) n t -> p j (n t)", j=PACK)
-            nc.sync.dma_start(out=raw[:], in_=channels_first[:, :, h * CHUNK_COLS : (h + 1) * CHUNK_COLS])
+        def load_block(b, h):
+            raw = raw_pool.tile([P, PACK, BLOCK_COLS], BF16, name="raw")
+            channels_first = x[b].rearrange("(j p) n t -> p j (n t)", p=P)
+            nc.sync.dma_start(out=raw[:], in_=channels_first[:, :, h * BLOCK_COLS : (h + 1) * BLOCK_COLS])
             raw_tiles[(b, h)] = raw
 
-        for h in range(CHUNKS):
-            load_chunk(0, h)
-        w_raw = prep.tile([P, 2, PACK, CH_OUT], BF16, name="w_raw")
-        nc.sync.dma_start(out=w_raw[:, 0], in_=w_cheb0.rearrange("(p j) o -> p j o", j=PACK))
-        nc.sync.dma_start(out=w_raw[:, 1], in_=w_cheb1.rearrange("(p j) o -> p j o", j=PACK))
-
-        gc_tiles = {}
-        xc, gn, xn, tx, gt, t1 = {}, {}, {}, {}, {}, {}
-
-        def regroup(item):
-            group, h = divmod(item, CHUNKS)
-            b, g = divmod(group, GROUPS)
-            if h == 0:
-                gc_tiles[group] = gc_pool.tile([P, T_GROUP * PLANE], BF16, name="gc", align_bytes=64)
-            planes = gc_tiles[group][:].rearrange("p (t q n j) -> p q n j t", t=T_GROUP, q=PACK, n=P, j=PACK)
-            piece = raw_tiles[(b, h)][:].rearrange("p j (n q t) -> p q n j t", q=PACK, t=TIMES)
-            nc.vector.tensor_copy(
-                out=planes[:, :, h * CHUNK_PN : (h + 1) * CHUNK_PN, :, :],
-                in_=piece[:, :, :, :, g * T_GROUP : (g + 1) * T_GROUP],
-            )
-
-        def channel_plane(i):
-            group, t = divmod(i, T_GROUP)
-            return gc_tiles[group][:, t * PLANE : (t + 1) * PLANE]
+        gc, xc, gn, xn, tx, gt, t1 = {}, {}, {}, {}, {}, {}, {}
 
         def quantise(pool, name, grouped):
             codes = pool.tile([P, PACK * P], U32, name=name + "_codes", align_bytes=64)
@@ -85,21 +69,29 @@ def tile_dynamicgraphspatialconv_pa_t_kernel(tc, x, adj_param, w_cheb0, w_cheb1,
             nc.vector.quantize_mx(out=codes[:].bitcast(FP8X4), scales=scales[:], in_=grouped)
             return codes, scales
 
+        def regroup(item):
+            group, h = divmod(item, PACK)
+            b, g = divmod(group, GROUPS)
+            gc[item] = gc_pool.tile([P, PLANE], BF16, name="gc", align_bytes=64)
+            nc.vector.tensor_copy(
+                out=gc[item][:].rearrange("p (t n j) -> p n j t", t=T_GROUP, n=P, j=PACK),
+                in_=raw_tiles[(b, h)][:].rearrange("p j (n t) -> p n j t", t=TIMES)[
+                    :, :, :, g * T_GROUP : (g + 1) * T_GROUP
+                ],
+            )
+
         def transpose_to_nodes(i):
-            words = channel_plane(i).bitcast(F32).rearrange("p (q n h) -> p q n h", q=PACK, n=P, h=2)
+            b, t = divmod(i, TIMES)
+            columns = z_tiles[b][:].rearrange("p g (n t) -> p g n t", t=TIMES)
             gn[i] = work.tile([P, PLANE], BF16, name="gn", align_bytes=64)
-            for h in range(2):
-                tr = tr_psum.tile([P, PACK, P], F32, name="tr")
-                for q in range(PACK):
-                    nc.tensor.transpose(tr[:, q, :], words[:, q, :, h], ident[:])
-                nc.scalar.copy(
-                    out=gn[i][:, h * PLANE // 2 : (h + 1) * PLANE // 2].rearrange(
-                        "p (e c q) -> p e c q", e=2, c=P, q=PACK
-                    ),
-                    in_=tr[:].rearrange("p q c -> p (q c)").bitcast(BF16).rearrange(
-                        "p (q c e) -> p e c q", q=PACK, c=P, e=2
-                    ),
-                )
+            for half in range(Z_GROUPS // BANK_GROUPS):
+                tr = tr_psum.tile([P, BANK_GROUPS * P], BF16, name="tr")
+                for k in range(BANK_GROUPS):
+                    nc.tensor.transpose(
+                        tr[:, k * P : (k + 1) * P], columns[:, half * BANK_GROUPS + k, :, t], ident_bf16[:]
+                    )
+                copy = nc.vector.tensor_copy if half == 0 else nc.scalar.copy
+                copy(out=gn[i][:, half * BANK_GROUPS * P : (half + 1) * BANK_GROUPS * P], in_=tr[:])
 
         def multiply_by_graph(i):
             codes, scales = xn[i]
@@ -122,23 +114,25 @@ def tile_dynamicgraphspatialconv_pa_t_kernel(tc, x, adj_param, w_cheb0, w_cheb1,
 
         def round_tx1(i):
             gt[i] = work.tile([P, PLANE], BF16, name="gt", align_bytes=64)
-            vector_banks = 2 if i - 1 + AHEAD < ITEMS else 3
             for v_block in range(PACK):
-                copy = nc.vector.tensor_copy if v_block < vector_banks else nc.scalar.copy
-                copy(
+                nc.scalar.copy(
                     out=gt[i][:, v_block * P * PACK : (v_block + 1) * P * PACK].rearrange("p (v j) -> p v j", j=PACK),
                     in_=tx[i][v_block][:].rearrange("p j v -> p v j"),
                 )
 
         def project(i):
             b, t = divmod(i, TIMES)
+            group, tt = divmod(i, T_GROUP)
             o_ps = o_psum.tile([P, PACK, CH_OUT], F32, name="o_ps")
-            for q in range(PACK):
-                n_cols = slice(q * P, (q + 1) * P)
-                for order, (codes, scales) in enumerate((xc[i], t1[i])):
+            for h in range(PACK):
+                operands = (
+                    (xc[group * PACK + h], slice(tt * P, (tt + 1) * P)),
+                    (t1[i], slice(h * P, (h + 1) * P)),
+                )
+                for order, ((codes, scales), n_cols) in enumerate(operands):
                     o_cols = slice(order * CH_OUT, (order + 1) * CH_OUT)
                     nc.tensor.matmul_mx(
-                        out=o_ps[:, q, :],
+                        out=o_ps[:, h, :],
                         lhsT=codes[:, n_cols].bitcast(FP8X4),
                         lhsT_scale=scales[:, n_cols],
                         rhs=w_codes[:, o_cols].bitcast(FP8X4),
@@ -146,105 +140,117 @@ def tile_dynamicgraphspatialconv_pa_t_kernel(tc, x, adj_param, w_cheb0, w_cheb1,
                         start=(order == 0),
                         stop=(order == 1),
                     )
-            o_sb = store.tile([P, PACK * CH_OUT], F32, name="o_sb")
-            nc.scalar.copy(out=o_sb[:], in_=o_ps[:].rearrange("p q o -> p (q o)"))
-            nc.sync.dma_start(out=out[b, t].rearrange("(p q) o -> p (q o)", q=PACK), in_=o_sb[:])
+            o_sb = store.tile([P, PACK, CH_OUT], F32, name="o_sb")
+            nc.scalar.copy(out=o_sb[:], in_=o_ps[:])
+            nc.sync.dma_start(out=out[b, t].rearrange("(h p) o -> p h o", p=P), in_=o_sb[:])
 
-        with tc.manual_schedule():
-            ident = const.tile([P, P], F32, name="ident")
-            make_identity(nc, ident[:])
-            off_diagonal = const.tile([P, P], F32, name="off_diagonal")
-            nc.vector.tensor_scalar(
-                out=off_diagonal[:], in0=ident[:], scalar1=-1.0, scalar2=1.0, op0=ALU.mult, op1=ALU.add
-            )
-            one = prep.tile([P, 1], F32, name="one")
-            nc.vector.memset(one[:], 1.0)
+        with tc.tile_pool(name="prep", bufs=1) as prep:
+            adj_raw = prep.tile([P, PACK, NODES], BF16, name="adj_raw")
+            nc.sync.dma_start(out=adj_raw[:], in_=adj_param.rearrange("(q p) m -> p q m", p=P))
+            w_raw = prep.tile([P, 2, PACK, CH_OUT], BF16, name="w_raw")
+            nc.sync.dma_start(out=w_raw[:, 0], in_=w_cheb0.rearrange("(j p) o -> p j o", p=P))
+            nc.sync.dma_start(out=w_raw[:, 1], in_=w_cheb1.rearrange("(j p) o -> p j o", p=P))
+            load_z(z_pool, 0)
+            for h in range(PACK):
+                load_block(0, h)
 
-            a = prep.tile([P, PACK, PACK, P], F32, name="a")
-            for q in range(PACK):
-                nc.scalar.activation(
-                    out=a[:, q],
-                    in_=adj_raw[:, q, :].rearrange("p (c k) -> p k c", k=PACK),
-                    func=ACT.Sigmoid,
+            with tc.manual_schedule():
+                ident = const.tile([P, P], F32, name="ident")
+                make_identity(nc, ident[:])
+                ident_bf16 = const.tile([P, P], BF16, name="ident_bf16")
+                make_identity(nc, ident_bf16[:])
+                off_diagonal = const.tile([P, P], F32, name="off_diagonal")
+                nc.vector.tensor_scalar(
+                    out=off_diagonal[:], in0=ident[:], scalar1=-1.0, scalar2=1.0, op0=ALU.mult, op1=ALU.add
                 )
-                nc.vector.tensor_tensor(out=a[:, q, q, :], in0=a[:, q, q, :], in1=off_diagonal[:], op=ALU.mult)
-            warm = prep.tile([P, 1], F32, name="warm")
-            nc.scalar.activation(out=warm[:], in_=one[:], func=ACT.Sqrt)
-            regroup(0)
-            two_a = prep.tile([P, PACK, PACK * P], F32, name="two_a")
-            two_deg = prep.tile([P, PACK], F32, name="two_deg")
-            for k in range(PACK):
-                a_t = tx_psum.tile([P, PACK, P], F32, name="tx")
+                one = prep.tile([P, 1], F32, name="one")
+                nc.vector.memset(one[:], 1.0)
+
+                a = prep.tile([P, PACK, PACK, P], F32, name="a")
                 for q in range(PACK):
-                    nc.tensor.transpose(a_t[:, q, :], a[:, q, k, :], ident[:])
+                    nc.scalar.activation(
+                        out=a[:, q].rearrange("p k c -> p (k c)"), in_=adj_raw[:, q, :], func=ACT.Sigmoid
+                    )
+                    nc.vector.tensor_tensor(out=a[:, q, q, :], in0=a[:, q, q, :], in1=off_diagonal[:], op=ALU.mult)
+                warm = prep.tile([P, 1], F32, name="warm")
+                nc.scalar.activation(out=warm[:], in_=one[:], func=ACT.Sqrt)
+                w_grouped = prep.tile([P, 2, CH_OUT, PACK], BF16, name="w_grouped", align_bytes=64)
+                nc.vector.tensor_copy(out=w_grouped[:], in_=w_raw[:].rearrange("p w j o -> p w o j"))
+                two_a = prep.tile([P, PACK, PACK * P], F32, name="two_a")
+                two_deg = prep.tile([P, PACK], F32, name="two_deg")
+                for k in range(PACK):
+                    a_t = tx_psum.tile([P, PACK, P], F32, name="tx")
+                    for q in range(PACK):
+                        nc.tensor.transpose(a_t[:, q, :], a[:, q, k, :], ident[:])
+                    nc.vector.tensor_tensor(
+                        out=two_a[:, k, :],
+                        in0=a[:, k].rearrange("p k c -> p (k c)"),
+                        in1=a_t[:].rearrange("p q c -> p (q c)"),
+                        op=ALU.add,
+                    )
+                    nc.scalar.activation(
+                        out=two_a[:, k, :], in_=two_a[:, k, :], func=ACT.Copy, accum_out=two_deg[:, k : k + 1]
+                    )
+                w_codes = const.tile([P, 2 * CH_OUT], U32, name="w_codes", align_bytes=64)
+                w_scales = const.tile([P, 2 * CH_OUT], U8, name="w_scales", align_bytes=64)
+                nc.vector.quantize_mx(
+                    out=w_codes[:].bitcast(FP8X4),
+                    scales=w_scales[:],
+                    in_=w_grouped[:].rearrange("p w o j -> p (w o j)"),
+                )
+                root = prep.tile([P, PACK], F32, name="root")
+                nc.scalar.activation(out=root[:], in_=two_deg[:], func=ACT.Sqrt, scale=0.5)
+                inv_root = prep.tile([P, PACK], F32, name="inv_root")
+                nc.vector.reciprocal(out=inv_root[:], in_=root[:])
+                row_factor = prep.tile([P, PACK], F32, name="row_factor")
+                nc.vector.tensor_scalar(
+                    out=row_factor[:], in0=inv_root[:], scalar1=-0.5, scalar2=None, op0=ALU.mult
+                )
+                for q in range(PACK):
+                    nc.scalar.activation(
+                        out=two_a[:, q, :], in_=two_a[:, q, :], func=ACT.Copy, scale=row_factor[:, q : q + 1]
+                    )
+                repeated = prep.tile([P, PACK, P], F32, name="repeated")
+                nc.vector.tensor_copy(out=repeated[:], in_=inv_root[:].unsqueeze(2).to_broadcast([P, PACK, P]))
+                column_factor = o_psum.tile([P, PACK, P], F32, name="o_ps")
+                for k in range(PACK):
+                    nc.tensor.transpose(column_factor[:, k, :], repeated[:, k, :], ident[:])
+                s_grouped = prep.tile([P, PACK * P, PACK], BF16, name="s_grouped", align_bytes=64)
                 nc.vector.tensor_tensor(
-                    out=two_a[:, k, :],
-                    in0=a[:, k].rearrange("p k c -> p (k c)"),
-                    in1=a_t[:].rearrange("p q c -> p (q c)"),
-                    op=ALU.add,
+                    out=s_grouped[:],
+                    in0=two_a[:].rearrange("p q v -> p v q"),
+                    in1=column_factor[:].rearrange("p k c -> p (k c)").unsqueeze(2).to_broadcast([P, PACK * P, PACK]),
+                    op=ALU.mult,
                 )
-                nc.scalar.activation(
-                    out=two_a[:, k, :], in_=two_a[:, k, :], func=ACT.Copy, accum_out=two_deg[:, k : k + 1]
+                s_codes = const.tile([P, PACK * P], U32, name="s_codes", align_bytes=64)
+                s_scales = const.tile([P, PACK * P], U8, name="s_scales", align_bytes=64)
+                nc.vector.quantize_mx(
+                    out=s_codes[:].bitcast(FP8X4),
+                    scales=s_scales[:],
+                    in_=s_grouped[:].rearrange("p v q -> p (v q)"),
                 )
-            regroup(1)
-            root = prep.tile([P, PACK], F32, name="root")
-            nc.scalar.activation(out=root[:], in_=two_deg[:], func=ACT.Sqrt, scale=0.5)
-            inv_root = prep.tile([P, PACK], F32, name="inv_root")
-            nc.vector.reciprocal(out=inv_root[:], in_=root[:])
-            row_factor = prep.tile([P, PACK], F32, name="row_factor")
-            nc.vector.tensor_scalar(out=row_factor[:], in0=inv_root[:], scalar1=-0.5, scalar2=None, op0=ALU.mult)
-            for q in range(PACK):
-                nc.scalar.activation(
-                    out=two_a[:, q, :], in_=two_a[:, q, :], func=ACT.Copy, scale=row_factor[:, q : q + 1]
-                )
-            repeated = prep.tile([P, PACK, P], F32, name="repeated")
-            nc.vector.tensor_copy(out=repeated[:], in_=inv_root[:].unsqueeze(2).to_broadcast([P, PACK, P]))
-            column_factor = o_psum.tile([P, PACK, P], F32, name="o_ps")
-            for k in range(PACK):
-                nc.tensor.transpose(column_factor[:, k, :], repeated[:, k, :], ident[:])
-            regroup(2)
-            regroup(3)
-            s_grouped = prep.tile([P, PACK * P, PACK], BF16, name="s_grouped", align_bytes=64)
-            nc.vector.tensor_tensor(
-                out=s_grouped[:],
-                in0=two_a[:].rearrange("p q v -> p v q"),
-                in1=column_factor[:].rearrange("p k c -> p (k c)").unsqueeze(2).to_broadcast([P, PACK * P, PACK]),
-                op=ALU.mult,
-            )
-            w_grouped = prep.tile([P, 2, CH_OUT, PACK], BF16, name="w_grouped", align_bytes=64)
-            nc.vector.tensor_copy(out=w_grouped[:], in_=w_raw[:].rearrange("p w j o -> p w o j"))
-            s_codes = const.tile([P, PACK * P], U32, name="s_codes", align_bytes=64)
-            s_scales = const.tile([P, PACK * P], U8, name="s_scales", align_bytes=64)
-            nc.vector.quantize_mx(
-                out=s_codes[:].bitcast(FP8X4), scales=s_scales[:], in_=s_grouped[:].rearrange("p v q -> p (v q)")
-            )
-            w_codes = const.tile([P, 2 * CH_OUT], U32, name="w_codes", align_bytes=64)
-            w_scales = const.tile([P, 2 * CH_OUT], U8, name="w_scales", align_bytes=64)
-            nc.vector.quantize_mx(
-                out=w_codes[:].bitcast(FP8X4),
-                scales=w_scales[:],
-                in_=w_grouped[:].rearrange("p w o j -> p (w o j)"),
-            )
 
-        for step in range(-2, STEPS):
-            first, second, third = step + 2, step + 1, step
+        load_z(ctx.enter_context(tc.tile_pool(name="z1", bufs=1)), 1)
+
+        for step in range(-2, STEPS + LAG):
+            first, second, third, fourth = step + 2, step + 1, step, step - LAG
             if 0 <= second < STEPS:
                 xn[second] = quantise(work, "xn", gn[second][:])
-            if 0 <= third:
-                t1[third] = quantise(work, "t1", gt[third][:])
+            if 0 <= third < STEPS:
+                t1[third] = quantise(t1_pool, "t1", gt[third][:])
             if first < STEPS:
                 transpose_to_nodes(first)
             if 0 <= second < STEPS:
                 multiply_by_graph(second)
-            if first < STEPS:
-                xc[first] = quantise(xc_pool, "xc", channel_plane(first))
+            item = step + 1
+            if 0 <= item - 1 < ITEMS:
+                xc[item - 1] = quantise(xc_pool, "xc", gc[item - 1][:])
+            if 0 <= item < ITEMS:
+                regroup(item)
+                group, h = divmod(item, PACK)
+                if group == GROUPS - 1:
+                    load_block(1, h)
             if 0 <= second < STEPS:
                 round_tx1(second)
-            if 0 <= third:
-                project(third)
-            item = step + AHEAD
-            if item < ITEMS:
-                regroup(item)
-                group, h = divmod(item, CHUNKS)
-                if group == GROUPS - 1:
-                    load_chunk(1, h)
+            if 0 <= fourth < STEPS:
+                project(fourth)

@@ -18,14 +18,10 @@ assert CHANNELS == P * PACK and NODES == P * PACK and CH_OUT == P
 
 STEPS = BATCH * TIMES
 PLANE = P * PACK * PACK
-BLOCK_COLS = P * TIMES
-Z_GROUPS = CHANNELS * PACK // P
-Z_LOADS = 4
-BANK_GROUPS = 8
+PAIRS = TIMES // 2
 T_GROUP = 4
 GROUPS = TIMES // T_GROUP
-ITEMS = BATCH * GROUPS * PACK
-LAG = 3
+ITEMS = GROUPS * PACK
 
 FLOPS = 2 * STEPS * (NODES * NODES * CHANNELS + 2 * NODES * CHANNELS * CH_OUT)
 
@@ -34,73 +30,67 @@ def tile_dynamicgraphspatialconv_pa_t_kernel(tc, x, adj_param, w_cheb0, w_cheb1,
     nc = tc.nc
     with ExitStack() as ctx:
         const = ctx.enter_context(tc.tile_pool(name="const", bufs=1))
-        z_pool = ctx.enter_context(tc.tile_pool(name="z0", bufs=1))
-        raw_pool = ctx.enter_context(tc.tile_pool(name="raw", bufs=PACK))
-        gc_pool = ctx.enter_context(tc.tile_pool(name="gc", bufs=3))
-        xc_pool = ctx.enter_context(tc.tile_pool(name="xc", bufs=2 * PACK + 1))
-        work = ctx.enter_context(tc.tile_pool(name="work", bufs=2))
-        t1_pool = ctx.enter_context(tc.tile_pool(name="t1", bufs=LAG + 2))
-        store = ctx.enter_context(tc.tile_pool(name="store", bufs=3))
+        raw_pool = ctx.enter_context(tc.tile_pool(name="raw", bufs=BATCH))
+        gn_pool = ctx.enter_context(tc.tile_pool(name="gn", bufs=3))
+        xn_pool = ctx.enter_context(tc.tile_pool(name="xn", bufs=ITEMS + PACK))
         tr_psum = ctx.enter_context(tc.psum_pool(name="tr_psum", bufs=3))
         tx_psum = ctx.enter_context(tc.psum_pool(name="tx_psum", bufs=4))
         o_psum = ctx.enter_context(tc.psum_pool(name="o_psum", bufs=1))
 
-        z_tiles, raw_tiles = {}, {}
+        raw, gc, xc, gn, xn, tx, gt, t1 = {}, {}, {}, {}, {}, {}, {}, {}
 
-        def load_z(pool, b):
-            z_tiles[b] = pool.tile([P, Z_GROUPS, BLOCK_COLS], BF16, name="z")
-            runs = x[b].rearrange("c n t -> (c n t)").rearrange("(g p f) -> p g f", g=Z_GROUPS, p=P)
-            share = Z_GROUPS // Z_LOADS
-            for k in range(Z_LOADS):
-                groups = slice(k * share, (k + 1) * share)
-                nc.sync.dma_start(out=z_tiles[b][:, groups, :], in_=runs[:, groups, :])
+        def load_batch(b):
+            raw[b] = raw_pool.tile([P, PACK, NODES * TIMES], BF16, name="raw")
+            for j in range(PACK):
+                nc.sync.dma_start(out=raw[b][:, j, :], in_=x[b, j * P : (j + 1) * P].rearrange("p n t -> p (n t)"))
 
-        def load_block(b, h):
-            raw = raw_pool.tile([P, PACK, BLOCK_COLS], BF16, name="raw")
-            channels_first = x[b].rearrange("(j p) n t -> p j (n t)", p=P)
-            nc.sync.dma_start(out=raw[:], in_=channels_first[:, :, h * BLOCK_COLS : (h + 1) * BLOCK_COLS])
-            raw_tiles[(b, h)] = raw
-
-        gc, xc, gn, xn, tx, gt, t1 = {}, {}, {}, {}, {}, {}, {}
-
-        def quantise(pool, name, grouped):
-            codes = pool.tile([P, PACK * P], U32, name=name + "_codes", align_bytes=64)
-            scales = pool.tile([P, PACK * P], U8, name=name + "_scales", align_bytes=64)
+        def quantise(pool, name, grouped, words):
+            codes = pool.tile([P, words], U32, name=name + "_codes", align_bytes=64)
+            scales = pool.tile([P, words], U8, name=name + "_scales", align_bytes=64)
             nc.vector.quantize_mx(out=codes[:].bitcast(FP8X4), scales=scales[:], in_=grouped)
             return codes, scales
 
-        def regroup(item):
-            group, h = divmod(item, PACK)
-            b, g = divmod(group, GROUPS)
-            gc[item] = gc_pool.tile([P, PLANE], BF16, name="gc", align_bytes=64)
+        def to_nodes(b, g, j):
+            words = raw[b][:, j, :].bitcast(F32).rearrange("p (q n w) -> p q n w", q=PACK, n=P, w=PAIRS)
+            gn[(b, g, j)] = gn_pool.tile([P, PLANE], BF16, name="gn", align_bytes=64)
+            for half in range(T_GROUP // 2):
+                tr = tr_psum.tile([P, PACK, P], F32, name="tr")
+                for q in range(PACK):
+                    nc.tensor.transpose(tr[:, q, :], words[:, q, :, g * T_GROUP // 2 + half], ident[:])
+                nc.any.tensor_copy(
+                    out=gn[(b, g, j)][:, half * PLANE // 2 : (half + 1) * PLANE // 2].rearrange(
+                        "p (e c q) -> p e c q", e=2, c=P, q=PACK
+                    ),
+                    in_=tr[:].rearrange("p q c -> p (q c)").bitcast(BF16).rearrange(
+                        "p (q c e) -> p e c q", q=PACK, c=P, e=2
+                    ),
+                )
+
+        def quantise_nodes(b, g, j):
+            xn[(b, g, j)] = quantise(xn_pool, "xn", gn[(b, g, j)][:], PACK * P)
+
+        def regroup(b, g, h):
+            gc[(b, g, h)] = gc_pool.tile([P, PLANE], BF16, name="gc", align_bytes=64)
             nc.vector.tensor_copy(
-                out=gc[item][:].rearrange("p (t n j) -> p n j t", t=T_GROUP, n=P, j=PACK),
-                in_=raw_tiles[(b, h)][:].rearrange("p j (n t) -> p n j t", t=TIMES)[
-                    :, :, :, g * T_GROUP : (g + 1) * T_GROUP
+                out=gc[(b, g, h)][:].rearrange("p (t n j) -> p n j t", t=T_GROUP, n=P, j=PACK),
+                in_=raw[b][:].rearrange("p j (n t) -> p n j t", t=TIMES)[
+                    :, h * P : (h + 1) * P, :, g * T_GROUP : (g + 1) * T_GROUP
                 ],
             )
 
-        def transpose_to_nodes(i):
-            b, t = divmod(i, TIMES)
-            columns = z_tiles[b][:].rearrange("p g (n t) -> p g n t", t=TIMES)
-            gn[i] = work.tile([P, PLANE], BF16, name="gn", align_bytes=64)
-            for half in range(Z_GROUPS // BANK_GROUPS):
-                tr = tr_psum.tile([P, BANK_GROUPS * P], BF16, name="tr")
-                for k in range(BANK_GROUPS):
-                    nc.tensor.transpose(
-                        tr[:, k * P : (k + 1) * P], columns[:, half * BANK_GROUPS + k, :, t], ident_bf16[:]
-                    )
-                copy = nc.vector.tensor_copy if half == 0 else nc.scalar.copy
-                copy(out=gn[i][:, half * BANK_GROUPS * P : (half + 1) * BANK_GROUPS * P], in_=tr[:])
+        def quantise_channels(b, g, h):
+            xc[(b, g, h)] = quantise(xc_pool, "xc", gc[(b, g, h)][:], PACK * P)
 
         def multiply_by_graph(i):
-            codes, scales = xn[i]
+            b, t = divmod(i, TIMES)
+            g, tt = divmod(t, T_GROUP)
+            c_cols = slice(tt * P, (tt + 1) * P)
             tx[i] = []
             for v_block in range(PACK):
                 bank = tx_psum.tile([P, PACK, P], F32, name="tx")
                 v_cols = slice(v_block * P, (v_block + 1) * P)
                 for j in range(PACK):
-                    c_cols = slice(j * P, (j + 1) * P)
+                    codes, scales = xn[(b, g, j)]
                     nc.tensor.matmul_mx(
                         out=bank[:, j, :],
                         lhsT=codes[:, c_cols].bitcast(FP8X4),
@@ -113,20 +103,20 @@ def tile_dynamicgraphspatialconv_pa_t_kernel(tc, x, adj_param, w_cheb0, w_cheb1,
                 tx[i].append(bank)
 
         def round_tx1(i):
-            gt[i] = work.tile([P, PLANE], BF16, name="gt", align_bytes=64)
+            gt[i] = gt_pool.tile([P, PLANE], BF16, name="gt", align_bytes=64)
             for v_block in range(PACK):
-                nc.scalar.copy(
+                nc.any.tensor_copy(
                     out=gt[i][:, v_block * P * PACK : (v_block + 1) * P * PACK].rearrange("p (v j) -> p v j", j=PACK),
                     in_=tx[i][v_block][:].rearrange("p j v -> p v j"),
                 )
 
         def project(i):
             b, t = divmod(i, TIMES)
-            group, tt = divmod(i, T_GROUP)
+            g, tt = divmod(t, T_GROUP)
             o_ps = o_psum.tile([P, PACK, CH_OUT], F32, name="o_ps")
             for h in range(PACK):
                 operands = (
-                    (xc[group * PACK + h], slice(tt * P, (tt + 1) * P)),
+                    (xc[(b, g, h)], slice(tt * P, (tt + 1) * P)),
                     (t1[i], slice(h * P, (h + 1) * P)),
                 )
                 for order, ((codes, scales), n_cols) in enumerate(operands):
@@ -141,7 +131,7 @@ def tile_dynamicgraphspatialconv_pa_t_kernel(tc, x, adj_param, w_cheb0, w_cheb1,
                         stop=(order == 1),
                     )
             o_sb = store.tile([P, PACK, CH_OUT], F32, name="o_sb")
-            nc.scalar.copy(out=o_sb[:], in_=o_ps[:])
+            nc.any.tensor_copy(out=o_sb[:], in_=o_ps[:])
             nc.sync.dma_start(out=out[b, t].rearrange("(h p) o -> p h o", p=P), in_=o_sb[:])
 
         with tc.tile_pool(name="prep", bufs=1) as prep:
@@ -150,107 +140,97 @@ def tile_dynamicgraphspatialconv_pa_t_kernel(tc, x, adj_param, w_cheb0, w_cheb1,
             w_raw = prep.tile([P, 2, PACK, CH_OUT], BF16, name="w_raw")
             nc.sync.dma_start(out=w_raw[:, 0], in_=w_cheb0.rearrange("(j p) o -> p j o", p=P))
             nc.sync.dma_start(out=w_raw[:, 1], in_=w_cheb1.rearrange("(j p) o -> p j o", p=P))
-            load_z(z_pool, 0)
-            for h in range(PACK):
-                load_block(0, h)
+            for b in range(BATCH):
+                load_batch(b)
 
-            with tc.manual_schedule():
-                ident = const.tile([P, P], F32, name="ident")
-                make_identity(nc, ident[:])
-                ident_bf16 = const.tile([P, P], BF16, name="ident_bf16")
-                make_identity(nc, ident_bf16[:])
-                off_diagonal = const.tile([P, P], F32, name="off_diagonal")
-                nc.vector.tensor_scalar(
-                    out=off_diagonal[:], in0=ident[:], scalar1=-1.0, scalar2=1.0, op0=ALU.mult, op1=ALU.add
-                )
-                one = prep.tile([P, 1], F32, name="one")
-                nc.vector.memset(one[:], 1.0)
+            ident = const.tile([P, P], F32, name="ident")
+            make_identity(nc, ident[:])
+            off_diagonal = const.tile([P, P], F32, name="off_diagonal")
+            nc.vector.tensor_scalar(
+                out=off_diagonal[:], in0=ident[:], scalar1=-1.0, scalar2=1.0, op0=ALU.mult, op1=ALU.add
+            )
 
-                a = prep.tile([P, PACK, PACK, P], F32, name="a")
+            w_grouped = prep.tile([P, 2, CH_OUT, PACK], BF16, name="w_grouped", align_bytes=64)
+            nc.vector.tensor_copy(out=w_grouped[:], in_=w_raw[:].rearrange("p w j o -> p w o j"))
+            w_codes, w_scales = quantise(const, "w", w_grouped[:].rearrange("p w o j -> p (w o j)"), 2 * CH_OUT)
+
+            a = prep.tile([P, PACK, PACK, P], F32, name="a")
+            for q in range(PACK):
+                nc.scalar.activation(out=a[:, q].rearrange("p k c -> p (k c)"), in_=adj_raw[:, q, :], func=ACT.Sigmoid)
+            warm = prep.tile([P, 1], F32, name="warm")
+            nc.scalar.activation(out=warm[:], in_=a[:, PACK - 1, 0, 0:1], func=ACT.Sqrt)
+            for q in range(PACK):
+                nc.vector.tensor_tensor(out=a[:, q, q, :], in0=a[:, q, q, :], in1=off_diagonal[:], op=ALU.mult)
+            two_a = prep.tile([P, PACK, PACK * P], F32, name="two_a")
+            two_deg = prep.tile([P, PACK], F32, name="two_deg")
+            for k in range(PACK):
+                a_t = tx_psum.tile([P, PACK, P], F32, name="tx")
                 for q in range(PACK):
-                    nc.scalar.activation(
-                        out=a[:, q].rearrange("p k c -> p (k c)"), in_=adj_raw[:, q, :], func=ACT.Sigmoid
-                    )
-                    nc.vector.tensor_tensor(out=a[:, q, q, :], in0=a[:, q, q, :], in1=off_diagonal[:], op=ALU.mult)
-                warm = prep.tile([P, 1], F32, name="warm")
-                nc.scalar.activation(out=warm[:], in_=one[:], func=ACT.Sqrt)
-                w_grouped = prep.tile([P, 2, CH_OUT, PACK], BF16, name="w_grouped", align_bytes=64)
-                nc.vector.tensor_copy(out=w_grouped[:], in_=w_raw[:].rearrange("p w j o -> p w o j"))
-                two_a = prep.tile([P, PACK, PACK * P], F32, name="two_a")
-                two_deg = prep.tile([P, PACK], F32, name="two_deg")
-                for k in range(PACK):
-                    a_t = tx_psum.tile([P, PACK, P], F32, name="tx")
-                    for q in range(PACK):
-                        nc.tensor.transpose(a_t[:, q, :], a[:, q, k, :], ident[:])
-                    nc.vector.tensor_tensor(
-                        out=two_a[:, k, :],
-                        in0=a[:, k].rearrange("p k c -> p (k c)"),
-                        in1=a_t[:].rearrange("p q c -> p (q c)"),
-                        op=ALU.add,
-                    )
-                    nc.scalar.activation(
-                        out=two_a[:, k, :], in_=two_a[:, k, :], func=ACT.Copy, accum_out=two_deg[:, k : k + 1]
-                    )
-                w_codes = const.tile([P, 2 * CH_OUT], U32, name="w_codes", align_bytes=64)
-                w_scales = const.tile([P, 2 * CH_OUT], U8, name="w_scales", align_bytes=64)
-                nc.vector.quantize_mx(
-                    out=w_codes[:].bitcast(FP8X4),
-                    scales=w_scales[:],
-                    in_=w_grouped[:].rearrange("p w o j -> p (w o j)"),
+                    nc.tensor.transpose(a_t[:, q, :], a[:, q, k, :], ident[:])
+                nc.vector.scalar_tensor_tensor(
+                    out=two_a[:, k, :],
+                    in0=a[:, k].rearrange("p k c -> p (k c)"),
+                    scalar=1.0,
+                    in1=a_t[:].rearrange("p q c -> p (q c)"),
+                    op0=ALU.mult,
+                    op1=ALU.add,
+                    accum_out=two_deg[:, k : k + 1],
                 )
-                root = prep.tile([P, PACK], F32, name="root")
-                nc.scalar.activation(out=root[:], in_=two_deg[:], func=ACT.Sqrt, scale=0.5)
-                inv_root = prep.tile([P, PACK], F32, name="inv_root")
-                nc.vector.reciprocal(out=inv_root[:], in_=root[:])
-                row_factor = prep.tile([P, PACK], F32, name="row_factor")
-                nc.vector.tensor_scalar(
-                    out=row_factor[:], in0=inv_root[:], scalar1=-0.5, scalar2=None, op0=ALU.mult
+            root = prep.tile([P, PACK], F32, name="root")
+            nc.scalar.activation(out=root[:], in_=two_deg[:], func=ACT.Sqrt, scale=0.5)
+            inv_root = prep.tile([P, PACK], F32, name="inv_root")
+            nc.vector.reciprocal(out=inv_root[:], in_=root[:])
+            row_factor = prep.tile([P, PACK], F32, name="row_factor")
+            nc.vector.tensor_scalar(out=row_factor[:], in0=inv_root[:], scalar1=-0.5, scalar2=None, op0=ALU.mult)
+            for q in range(PACK):
+                nc.scalar.activation(
+                    out=two_a[:, q, :], in_=two_a[:, q, :], func=ACT.Copy, scale=row_factor[:, q : q + 1]
                 )
-                for q in range(PACK):
-                    nc.scalar.activation(
-                        out=two_a[:, q, :], in_=two_a[:, q, :], func=ACT.Copy, scale=row_factor[:, q : q + 1]
-                    )
-                repeated = prep.tile([P, PACK, P], F32, name="repeated")
-                nc.vector.tensor_copy(out=repeated[:], in_=inv_root[:].unsqueeze(2).to_broadcast([P, PACK, P]))
-                column_factor = o_psum.tile([P, PACK, P], F32, name="o_ps")
-                for k in range(PACK):
-                    nc.tensor.transpose(column_factor[:, k, :], repeated[:, k, :], ident[:])
-                s_grouped = prep.tile([P, PACK * P, PACK], BF16, name="s_grouped", align_bytes=64)
-                nc.vector.tensor_tensor(
-                    out=s_grouped[:],
-                    in0=two_a[:].rearrange("p q v -> p v q"),
-                    in1=column_factor[:].rearrange("p k c -> p (k c)").unsqueeze(2).to_broadcast([P, PACK * P, PACK]),
-                    op=ALU.mult,
-                )
-                s_codes = const.tile([P, PACK * P], U32, name="s_codes", align_bytes=64)
-                s_scales = const.tile([P, PACK * P], U8, name="s_scales", align_bytes=64)
-                nc.vector.quantize_mx(
-                    out=s_codes[:].bitcast(FP8X4),
-                    scales=s_scales[:],
-                    in_=s_grouped[:].rearrange("p v q -> p (v q)"),
-                )
+            repeated = prep.tile([P, PACK, P], F32, name="repeated")
+            nc.vector.tensor_copy(out=repeated[:], in_=inv_root[:].unsqueeze(2).to_broadcast([P, PACK, P]))
+            column_factor = o_psum.tile([P, PACK, P], F32, name="o_ps")
+            for k in range(PACK):
+                nc.tensor.transpose(column_factor[:, k, :], repeated[:, k, :], ident[:])
+            s_grouped = prep.tile([P, PACK * P, PACK], BF16, name="s_grouped", align_bytes=64)
+            nc.vector.tensor_tensor(
+                out=s_grouped[:],
+                in0=two_a[:].rearrange("p q v -> p v q"),
+                in1=column_factor[:].rearrange("p k c -> p (k c)").unsqueeze(2).to_broadcast([P, PACK * P, PACK]),
+                op=ALU.mult,
+            )
+            s_codes, s_scales = quantise(const, "s", s_grouped[:].rearrange("p v q -> p (v q)"), PACK * P)
 
-        load_z(ctx.enter_context(tc.tile_pool(name="z1", bufs=1)), 1)
+        gc_pool = ctx.enter_context(tc.tile_pool(name="gc", bufs=3))
+        xc_pool = ctx.enter_context(tc.tile_pool(name="xc", bufs=2 * PACK + 2))
+        gt_pool = ctx.enter_context(tc.tile_pool(name="gt", bufs=3))
+        t1_pool = ctx.enter_context(tc.tile_pool(name="t1", bufs=3))
+        store = ctx.enter_context(tc.tile_pool(name="store", bufs=3))
 
-        for step in range(-2, STEPS + LAG):
-            first, second, third, fourth = step + 2, step + 1, step, step - LAG
-            if 0 <= second < STEPS:
-                xn[second] = quantise(work, "xn", gn[second][:])
-            if 0 <= third < STEPS:
-                t1[third] = quantise(t1_pool, "t1", gt[third][:])
-            if first < STEPS:
-                transpose_to_nodes(first)
-            if 0 <= second < STEPS:
-                multiply_by_graph(second)
-            item = step + 1
-            if 0 <= item - 1 < ITEMS:
-                xc[item - 1] = quantise(xc_pool, "xc", gc[item - 1][:])
-            if 0 <= item < ITEMS:
-                regroup(item)
-                group, h = divmod(item, PACK)
-                if group == GROUPS - 1:
-                    load_block(1, h)
-            if 0 <= second < STEPS:
-                round_tx1(second)
-            if 0 <= fourth < STEPS:
-                project(fourth)
+        by_piece = [(0, g, j) for j in range(PACK) for g in range(GROUPS)]
+        for n, item in enumerate(by_piece):
+            to_nodes(*item)
+            if n > 0:
+                quantise_nodes(*by_piece[n - 1])
+        quantise_nodes(*by_piece[-1])
+        by_group = [(b, g, k) for b in range(BATCH) for g in range(GROUPS) for k in range(PACK)]
+        AHEAD = PACK - 1
+        for n in range(AHEAD):
+            regroup(*by_group[n])
+            if n > 0:
+                quantise_channels(*by_group[n - 1])
+        for i in range(STEPS + 1):
+            if i < STEPS:
+                multiply_by_graph(i)
+            if i + AHEAD < len(by_group):
+                regroup(*by_group[i + AHEAD])
+            if i + AHEAD - 1 < len(by_group):
+                quantise_channels(*by_group[i + AHEAD - 1])
+            if i > 0:
+                t1[i - 1] = quantise(t1_pool, "t1", gt[i - 1][:], PACK * P)
+                project(i - 1)
+            if i < STEPS:
+                round_tx1(i)
+            if i < ITEMS:
+                to_nodes(*by_group[ITEMS + i])
+            if 0 < i <= ITEMS:
+                quantise_nodes(*by_group[ITEMS + i - 1])

@@ -44,10 +44,16 @@ def tile_dynamicgraphspatialconv_pa_t_kernel(tc, x, adj_param, w_cheb0, w_cheb1,
             for j in range(PACK):
                 nc.sync.dma_start(out=raw[b][:, j, :], in_=x[b, j * P : (j + 1) * P].rearrange("p n t -> p (n t)"))
 
-        def quantise(pool, name, grouped, words):
+        def quantise(pool, name, grouped, words, calls=1):
             codes = pool.tile([P, words], U32, name=name + "_codes", align_bytes=64)
             scales = pool.tile([P, words], U8, name=name + "_scales", align_bytes=64)
-            nc.vector.quantize_mx(out=codes[:].bitcast(FP8X4), scales=scales[:], in_=grouped)
+            for n in range(calls):
+                part = slice(n * words // calls, (n + 1) * words // calls)
+                nc.vector.quantize_mx(
+                    out=codes[:, part].bitcast(FP8X4),
+                    scales=scales[:, part],
+                    in_=grouped[:, part.start * PACK : part.stop * PACK],
+                )
             return codes, scales
 
         def to_nodes(b, g, j):
@@ -110,11 +116,10 @@ def tile_dynamicgraphspatialconv_pa_t_kernel(tc, x, adj_param, w_cheb0, w_cheb1,
                     in_=tx[i][v_block][:].rearrange("p j v -> p v j"),
                 )
 
-        def project(i):
+        def project(i, o_ps, blocks):
             b, t = divmod(i, TIMES)
             g, tt = divmod(t, T_GROUP)
-            o_ps = o_psum.tile([P, PACK, CH_OUT], F32, name="o_ps")
-            for h in range(PACK):
+            for n, h in enumerate(blocks):
                 operands = (
                     (xc[(b, g, h)], slice(tt * P, (tt + 1) * P)),
                     (t1[i], slice(h * P, (h + 1) * P)),
@@ -122,7 +127,7 @@ def tile_dynamicgraphspatialconv_pa_t_kernel(tc, x, adj_param, w_cheb0, w_cheb1,
                 for order, ((codes, scales), n_cols) in enumerate(operands):
                     o_cols = slice(order * CH_OUT, (order + 1) * CH_OUT)
                     nc.tensor.matmul_mx(
-                        out=o_ps[:, h, :],
+                        out=o_ps[:, n, :],
                         lhsT=codes[:, n_cols].bitcast(FP8X4),
                         lhsT_scale=scales[:, n_cols],
                         rhs=w_codes[:, o_cols].bitcast(FP8X4),
@@ -130,9 +135,13 @@ def tile_dynamicgraphspatialconv_pa_t_kernel(tc, x, adj_param, w_cheb0, w_cheb1,
                         start=(order == 0),
                         stop=(order == 1),
                     )
-            o_sb = store.tile([P, PACK, CH_OUT], F32, name="o_sb")
+            o_sb = store.tile([P, len(blocks), CH_OUT], F32, name="o_sb")
             nc.any.tensor_copy(out=o_sb[:], in_=o_ps[:])
-            nc.sync.dma_start(out=out[b, t].rearrange("(h p) o -> p h o", p=P), in_=o_sb[:])
+            nc.sync.dma_start(
+                out=out[b, t, blocks[0] * P : (blocks[-1] + 1) * P].rearrange("(h p) o -> p h o", p=P), in_=o_sb[:]
+            )
+
+        by_piece = [(0, g, j) for j in range(PACK) for g in range(GROUPS)]
 
         with tc.tile_pool(name="prep", bufs=1) as prep:
             adj_raw = prep.tile([P, PACK, NODES], BF16, name="adj_raw")
@@ -163,34 +172,38 @@ def tile_dynamicgraphspatialconv_pa_t_kernel(tc, x, adj_param, w_cheb0, w_cheb1,
                 nc.vector.tensor_tensor(out=a[:, q, q, :], in0=a[:, q, q, :], in1=off_diagonal[:], op=ALU.mult)
             two_a = prep.tile([P, PACK, PACK * P], F32, name="two_a")
             two_deg = prep.tile([P, PACK], F32, name="two_deg")
-            for k in range(PACK):
-                a_t = tx_psum.tile([P, PACK, P], F32, name="tx")
-                for q in range(PACK):
-                    nc.tensor.transpose(a_t[:, q, :], a[:, q, k, :], ident[:])
-                nc.vector.scalar_tensor_tensor(
-                    out=two_a[:, k, :],
-                    in0=a[:, k].rearrange("p k c -> p (k c)"),
-                    scalar=1.0,
-                    in1=a_t[:].rearrange("p q c -> p (q c)"),
-                    op0=ALU.mult,
-                    op1=ALU.add,
-                    accum_out=two_deg[:, k : k + 1],
-                )
+            with tc.manual_schedule(engines={mybir.EngineType.PE}):
+                for k in range(PACK):
+                    a_t = tx_psum.tile([P, PACK, P], F32, name="tx")
+                    for q in range(PACK):
+                        nc.tensor.transpose(a_t[:, q, :], a[:, q, k, :], ident[:])
+                    nc.vector.scalar_tensor_tensor(
+                        out=two_a[:, k, :],
+                        in0=a[:, k].rearrange("p k c -> p (k c)"),
+                        scalar=1.0,
+                        in1=a_t[:].rearrange("p q c -> p (q c)"),
+                        op0=ALU.mult,
+                        op1=ALU.add,
+                        accum_out=two_deg[:, k : k + 1],
+                    )
+                for item in by_piece[:GROUPS]:
+                    to_nodes(*item)
             root = prep.tile([P, PACK], F32, name="root")
             nc.scalar.activation(out=root[:], in_=two_deg[:], func=ACT.Sqrt, scale=0.5)
             inv_root = prep.tile([P, PACK], F32, name="inv_root")
             nc.vector.reciprocal(out=inv_root[:], in_=root[:])
-            row_factor = prep.tile([P, PACK], F32, name="row_factor")
-            nc.vector.tensor_scalar(out=row_factor[:], in0=inv_root[:], scalar1=-0.5, scalar2=None, op0=ALU.mult)
             for q in range(PACK):
-                nc.scalar.activation(
-                    out=two_a[:, q, :], in_=two_a[:, q, :], func=ACT.Copy, scale=row_factor[:, q : q + 1]
+                nc.gpsimd.tensor_scalar(
+                    out=two_a[:, q, :],
+                    in0=two_a[:, q, :],
+                    scalar1=inv_root[:, q : q + 1],
+                    scalar2=-0.5,
+                    op0=ALU.mult,
+                    op1=ALU.mult,
                 )
-            repeated = prep.tile([P, PACK, P], F32, name="repeated")
-            nc.vector.tensor_copy(out=repeated[:], in_=inv_root[:].unsqueeze(2).to_broadcast([P, PACK, P]))
             column_factor = o_psum.tile([P, PACK, P], F32, name="o_ps")
             for k in range(PACK):
-                nc.tensor.transpose(column_factor[:, k, :], repeated[:, k, :], ident[:])
+                nc.tensor.transpose(column_factor[:, k, :], inv_root[:, k : k + 1].to_broadcast([P, P]), ident[:])
             s_grouped = prep.tile([P, PACK * P, PACK], BF16, name="s_grouped", align_bytes=64)
             nc.vector.tensor_tensor(
                 out=s_grouped[:],
@@ -206,9 +219,9 @@ def tile_dynamicgraphspatialconv_pa_t_kernel(tc, x, adj_param, w_cheb0, w_cheb1,
         t1_pool = ctx.enter_context(tc.tile_pool(name="t1", bufs=3))
         store = ctx.enter_context(tc.tile_pool(name="store", bufs=3))
 
-        by_piece = [(0, g, j) for j in range(PACK) for g in range(GROUPS)]
         for n, item in enumerate(by_piece):
-            to_nodes(*item)
+            if n >= GROUPS:
+                to_nodes(*item)
             if n > 0:
                 quantise_nodes(*by_piece[n - 1])
         quantise_nodes(*by_piece[-1])
@@ -218,6 +231,7 @@ def tile_dynamicgraphspatialconv_pa_t_kernel(tc, x, adj_param, w_cheb0, w_cheb1,
             regroup(*by_group[n])
             if n > 0:
                 quantise_channels(*by_group[n - 1])
+        items_at = {m * (STEPS - T_GROUP) // ITEMS: by_group[ITEMS + m] for m in range(ITEMS)}
         for i in range(STEPS + 1):
             if i < STEPS:
                 multiply_by_graph(i)
@@ -226,11 +240,15 @@ def tile_dynamicgraphspatialconv_pa_t_kernel(tc, x, adj_param, w_cheb0, w_cheb1,
             if i + AHEAD - 1 < len(by_group):
                 quantise_channels(*by_group[i + AHEAD - 1])
             if i > 0:
-                t1[i - 1] = quantise(t1_pool, "t1", gt[i - 1][:], PACK * P)
-                project(i - 1)
+                halves = 2 if i == STEPS else 1
+                t1[i - 1] = quantise(t1_pool, "t1", gt[i - 1][:], PACK * P, calls=halves)
+                for n in range(halves):
+                    blocks = range(n * PACK // halves, (n + 1) * PACK // halves)
+                    pool, tag = (o_psum, "o_ps") if n == 0 else (tx_psum, "tx")
+                    project(i - 1, pool.tile([P, len(blocks), CH_OUT], F32, name=tag), blocks)
             if i < STEPS:
                 round_tx1(i)
-            if i < ITEMS:
-                to_nodes(*by_group[ITEMS + i])
-            if 0 < i <= ITEMS:
-                quantise_nodes(*by_group[ITEMS + i - 1])
+            if i in items_at:
+                to_nodes(*items_at[i])
+            if i - 1 in items_at:
+                quantise_nodes(*items_at[i - 1])

from contextlib import ExitStack

import concourse.mybir as mybir
from concourse.masks import make_identity

BF16 = mybir.dt.bfloat16
F32 = mybir.dt.float32
U32 = mybir.dt.uint32
U8 = mybir.dt.uint8
FP8X4 = mybir.dt.float8_e4m3fn_x4
ACT = mybir.ActivationFunctionType
ALU = mybir.AluOpType

P = 128
PACK = 4
BATCH, CHANNELS, NODES, TIMES, CH_OUT = 2, 512, 512, 12, 128
assert CHANNELS == P * PACK and NODES == P * PACK and CH_OUT == P

STEPS = BATCH * TIMES
PLANE = P * PACK * PACK
PAIRS = TIMES // 2
T_GROUP = 4
GROUPS = TIMES // T_GROUP
ITEMS = GROUPS * PACK

FLOPS = 2 * STEPS * (NODES * NODES * CHANNELS + 2 * NODES * CHANNELS * CH_OUT)


def tile_dynamicgraphspatialconv_pa_t_kernel(tc, x, adj_param, w_cheb0, w_cheb1, out):
    nc = tc.nc
    with ExitStack() as ctx:
        const = ctx.enter_context(tc.tile_pool(name="const", bufs=1))
        raw_pool = ctx.enter_context(tc.tile_pool(name="raw", bufs=BATCH))
        gn_pool = ctx.enter_context(tc.tile_pool(name="gn", bufs=3))
        xn_pool = ctx.enter_context(tc.tile_pool(name="xn", bufs=ITEMS + PACK))
        tr_psum = ctx.enter_context(tc.psum_pool(name="tr_psum", bufs=3))
        tx_psum = ctx.enter_context(tc.psum_pool(name="tx_psum", bufs=4))
        o_psum = ctx.enter_context(tc.psum_pool(name="o_psum", bufs=1))

        raw, gc, xc, gn, xn, tx, gt, t1 = {}, {}, {}, {}, {}, {}, {}, {}

        def load_batch(b):
            raw[b] = raw_pool.tile([P, PACK, NODES * TIMES], BF16, name="raw")
            for j in range(PACK):
                nc.sync.dma_start(out=raw[b][:, j, :], in_=x[b, j * P : (j + 1) * P].rearrange("p n t -> p (n t)"))

        def quantise(pool, name, grouped, words, calls=1):
            codes = pool.tile([P, words], U32, name=name + "_codes", align_bytes=64)
            scales = pool.tile([P, words], U8, name=name + "_scales", align_bytes=64)
            for n in range(calls):
                part = slice(n * words // calls, (n + 1) * words // calls)
                nc.vector.quantize_mx(
                    out=codes[:, part].bitcast(FP8X4),
                    scales=scales[:, part],
                    in_=grouped[:, part.start * PACK : part.stop * PACK],
                )
            return codes, scales

        def to_nodes(b, g, j):
            words = raw[b][:, j, :].bitcast(F32).rearrange("p (q n w) -> p q n w", q=PACK, n=P, w=PAIRS)
            gn[(b, g, j)] = gn_pool.tile([P, PLANE], BF16, name="gn", align_bytes=64)
            for half in range(T_GROUP // 2):
                tr = tr_psum.tile([P, PACK, P], F32, name="tr")
                for q in range(PACK):
                    nc.tensor.transpose(tr[:, q, :], words[:, q, :, g * T_GROUP // 2 + half], ident[:])
                nc.any.tensor_copy(
                    out=gn[(b, g, j)][:, half * PLANE // 2 : (half + 1) * PLANE // 2].rearrange(
                        "p (e c q) -> p e c q", e=2, c=P, q=PACK
                    ),
                    in_=tr[:].rearrange("p q c -> p (q c)").bitcast(BF16).rearrange(
                        "p (q c e) -> p e c q", q=PACK, c=P, e=2
                    ),
                )

        def quantise_nodes(b, g, j):
            xn[(b, g, j)] = quantise(xn_pool, "xn", gn[(b, g, j)][:], PACK * P)

        def regroup(b, g, h):
            gc[(b, g, h)] = gc_pool.tile([P, PLANE], BF16, name="gc", align_bytes=64)
            nc.vector.tensor_copy(
                out=gc[(b, g, h)][:].rearrange("p (t n j) -> p n j t", t=T_GROUP, n=P, j=PACK),
                in_=raw[b][:].rearrange("p j (n t) -> p n j t", t=TIMES)[
                    :, h * P : (h + 1) * P, :, g * T_GROUP : (g + 1) * T_GROUP
                ],
            )

        def quantise_channels(b, g, h):
            xc[(b, g, h)] = quantise(xc_pool, "xc", gc[(b, g, h)][:], PACK * P)

        def multiply_by_graph(i):
            b, t = divmod(i, TIMES)
            g, tt = divmod(t, T_GROUP)
            c_cols = slice(tt * P, (tt + 1) * P)
            tx[i] = []
            for v_block in range(PACK):
                bank = tx_psum.tile([P, PACK, P], F32, name="tx")
                v_cols = slice(v_block * P, (v_block + 1) * P)
                for j in range(PACK):
                    codes, scales = xn[(b, g, j)]
                    nc.tensor.matmul_mx(
                        out=bank[:, j, :],
                        lhsT=codes[:, c_cols].bitcast(FP8X4),
                        lhsT_scale=scales[:, c_cols],
                        rhs=s_codes[:, v_cols].bitcast(FP8X4),
                        rhs_scale=s_scales[:, v_cols],
                        start=True,
                        stop=True,
                    )
                tx[i].append(bank)

        def round_tx1(i):
            gt[i] = gt_pool.tile([P, PLANE], BF16, name="gt", align_bytes=64)
            for v_block in range(PACK):
                nc.any.tensor_copy(
                    out=gt[i][:, v_block * P * PACK : (v_block + 1) * P * PACK].rearrange("p (v j) -> p v j", j=PACK),
                    in_=tx[i][v_block][:].rearrange("p j v -> p v j"),
                )

        def project(i, o_ps, blocks):
            b, t = divmod(i, TIMES)
            g, tt = divmod(t, T_GROUP)
            for n, h in enumerate(blocks):
                operands = (
                    (xc[(b, g, h)], slice(tt * P, (tt + 1) * P)),
                    (t1[i], slice(h * P, (h + 1) * P)),
                )
                for order, ((codes, scales), n_cols) in enumerate(operands):
                    o_cols = slice(order * CH_OUT, (order + 1) * CH_OUT)
                    nc.tensor.matmul_mx(
                        out=o_ps[:, n, :],
                        lhsT=codes[:, n_cols].bitcast(FP8X4),
                        lhsT_scale=scales[:, n_cols],
                        rhs=w_codes[:, o_cols].bitcast(FP8X4),
                        rhs_scale=w_scales[:, o_cols],
                        start=(order == 0),
                        stop=(order == 1),
                    )
            o_sb = store.tile([P, len(blocks), CH_OUT], F32, name="o_sb")
            nc.any.tensor_copy(out=o_sb[:], in_=o_ps[:])
            nc.sync.dma_start(
                out=out[b, t, blocks[0] * P : (blocks[-1] + 1) * P].rearrange("(h p) o -> p h o", p=P), in_=o_sb[:]
            )

        by_piece = [(0, g, j) for j in range(PACK) for g in range(GROUPS)]

        with tc.tile_pool(name="prep", bufs=1) as prep:
            adj_raw = prep.tile([P, PACK, NODES], BF16, name="adj_raw")
            nc.sync.dma_start(out=adj_raw[:], in_=adj_param.rearrange("(q p) m -> p q m", p=P))
            w_raw = prep.tile([P, 2, PACK, CH_OUT], BF16, name="w_raw")
            nc.sync.dma_start(out=w_raw[:, 0], in_=w_cheb0.rearrange("(j p) o -> p j o", p=P))
            nc.sync.dma_start(out=w_raw[:, 1], in_=w_cheb1.rearrange("(j p) o -> p j o", p=P))
            for b in range(BATCH):
                load_batch(b)

            ident = const.tile([P, P], F32, name="ident")
            make_identity(nc, ident[:])
            off_diagonal = const.tile([P, P], F32, name="off_diagonal")
            nc.vector.tensor_scalar(
                out=off_diagonal[:], in0=ident[:], scalar1=-1.0, scalar2=1.0, op0=ALU.mult, op1=ALU.add
            )

            w_grouped = prep.tile([P, 2, CH_OUT, PACK], BF16, name="w_grouped", align_bytes=64)
            nc.vector.tensor_copy(out=w_grouped[:], in_=w_raw[:].rearrange("p w j o -> p w o j"))
            w_codes, w_scales = quantise(const, "w", w_grouped[:].rearrange("p w o j -> p (w o j)"), 2 * CH_OUT)

            a = prep.tile([P, PACK, PACK, P], F32, name="a")
            for q in range(PACK):
                nc.scalar.activation(out=a[:, q].rearrange("p k c -> p (k c)"), in_=adj_raw[:, q, :], func=ACT.Sigmoid)
            warm = prep.tile([P, 1], F32, name="warm")
            nc.scalar.activation(out=warm[:], in_=a[:, PACK - 1, 0, 0:1], func=ACT.Sqrt)
            for q in range(PACK):
                nc.vector.tensor_tensor(out=a[:, q, q, :], in0=a[:, q, q, :], in1=off_diagonal[:], op=ALU.mult)
            two_a = prep.tile([P, PACK, PACK * P], F32, name="two_a")
            two_deg = prep.tile([P, PACK], F32, name="two_deg")
            with tc.manual_schedule(engines={mybir.EngineType.PE}):
                for k in range(PACK):
                    a_t = tx_psum.tile([P, PACK, P], F32, name="tx")
                    for q in range(PACK):
                        nc.tensor.transpose(a_t[:, q, :], a[:, q, k, :], ident[:])
                    nc.vector.scalar_tensor_tensor(
                        out=two_a[:, k, :],
                        in0=a[:, k].rearrange("p k c -> p (k c)"),
                        scalar=1.0,
                        in1=a_t[:].rearrange("p q c -> p (q c)"),
                        op0=ALU.mult,
                        op1=ALU.add,
                        accum_out=two_deg[:, k : k + 1],
                    )
                for item in by_piece[:GROUPS]:
                    to_nodes(*item)
            root = prep.tile([P, PACK], F32, name="root")
            nc.scalar.activation(out=root[:], in_=two_deg[:], func=ACT.Sqrt, scale=0.5)
            inv_root = prep.tile([P, PACK], F32, name="inv_root")
            nc.vector.reciprocal(out=inv_root[:], in_=root[:])
            for q in range(PACK):
                nc.gpsimd.tensor_scalar(
                    out=two_a[:, q, :],
                    in0=two_a[:, q, :],
                    scalar1=inv_root[:, q : q + 1],
                    scalar2=-0.5,
                    op0=ALU.mult,
                    op1=ALU.mult,
                )
            column_factor = o_psum.tile([P, PACK, P], F32, name="o_ps")
            for k in range(PACK):
                nc.tensor.transpose(column_factor[:, k, :], inv_root[:, k : k + 1].to_broadcast([P, P]), ident[:])
            s_grouped = prep.tile([P, PACK * P, PACK], BF16, name="s_grouped", align_bytes=64)
            nc.vector.tensor_tensor(
                out=s_grouped[:],
                in0=two_a[:].rearrange("p q v -> p v q"),
                in1=column_factor[:].rearrange("p k c -> p (k c)").unsqueeze(2).to_broadcast([P, PACK * P, PACK]),
                op=ALU.mult,
            )
            s_codes, s_scales = quantise(const, "s", s_grouped[:].rearrange("p v q -> p (v q)"), PACK * P)

        gc_pool = ctx.enter_context(tc.tile_pool(name="gc", bufs=3))
        xc_pool = ctx.enter_context(tc.tile_pool(name="xc", bufs=2 * PACK + 2))
        gt_pool = ctx.enter_context(tc.tile_pool(name="gt", bufs=3))
        t1_pool = ctx.enter_context(tc.tile_pool(name="t1", bufs=3))
        store = ctx.enter_context(tc.tile_pool(name="store", bufs=3))

        for n, item in enumerate(by_piece):
            if n >= GROUPS:
                to_nodes(*item)
            if n > 0:
                quantise_nodes(*by_piece[n - 1])
        quantise_nodes(*by_piece[-1])
        by_group = [(b, g, k) for b in range(BATCH) for g in range(GROUPS) for k in range(PACK)]
        AHEAD = PACK - 1
        for n in range(AHEAD):
            regroup(*by_group[n])
            if n > 0:
                quantise_channels(*by_group[n - 1])
        items_at = {m * (STEPS - T_GROUP) // ITEMS: by_group[ITEMS + m] for m in range(ITEMS)}
        for i in range(STEPS + 1):
            if i < STEPS:
                multiply_by_graph(i)
            if i + AHEAD < len(by_group):
                regroup(*by_group[i + AHEAD])
            if i + AHEAD - 1 < len(by_group):
                quantise_channels(*by_group[i + AHEAD - 1])
            if i > 0:
                halves = 2 if i == STEPS else 1
                t1[i - 1] = quantise(t1_pool, "t1", gt[i - 1][:], PACK * P, calls=halves)
                for n in range(halves):
                    blocks = range(n * PACK // halves, (n + 1) * PACK // halves)
                    pool, tag = (o_psum, "o_ps") if n == 0 else (tx_psum, "tx")
                    project(i - 1, pool.tile([P, len(blocks), CH_OUT], F32, name=tag), blocks)
            if i < STEPS:
                round_tx1(i)
            if i in items_at:
                to_nodes(*items_at[i])
            if i - 1 in items_at:
                quantise_nodes(*items_at[i - 1])
